import numpy as np
import ml_dtypes

BF16 = ml_dtypes.bfloat16


def bf(x):
    return np.asarray(x, np.float32).astype(BF16)


def f32(x):
    return np.asarray(x, np.float32)


def f64(x):
    return np.asarray(x).astype(np.float64)


def striped(idx):
    return np.tile(idx.reshape(-1, 16).T, (8, 1))


C, S, N = 1024, 256, 128
PREDICT_GAP, RELATION_GAP, CONF = 0.1, 0.05, 4.0


def setup_inputs():
    u = np.random.rand(C, N)
    sure = np.random.rand(C, N) < CONF / C
    p = np.where(sure, 0.7 + 0.3 * u, 0.5 * u)
    prob = 0.3 + 0.4 * np.random.rand(C, 1)
    r = np.random.rand(C, C)
    np.fill_diagonal(r, 0.5)
    v = np.random.rand(C, C)
    shift = np.where(r < 1.0 / 3.0, -0.1 - 0.2 * v, np.where(r > 2.0 / 3.0, 0.1 + 0.2 * v, 0.03 * (2.0 * v - 1.0)))
    adj = prob.T + shift
    base = 0.5 * np.random.rand(C, S)
    return {"base": f32(base), "p": f32(p), "adj": f32(adj), "prob": f32(prob), "offs": striped(np.random.permutation(S)[:N])}


def reference(base, p, adj, prob, offs):
    idx = offs[:16].T.reshape(-1)
    p, adj, row = f64(p), f64(adj), f64(prob).T
    e = np.where(p > 0.5 + PREDICT_GAP, 1.0, 0.0)
    inc = np.where(adj > row + RELATION_GAP, 1.0, 0.0)
    dec = np.where(adj < row - RELATION_GAP, 1.0, 0.0)
    w = inc * adj - dec * (1.0 - adj)
    num = p + w.T @ (e * p) + dec.T @ e
    rel = 1.0 + e.sum(axis=0, keepdims=True) - e
    out = f64(base).copy()
    out[:, idx] = num * (1.0 / rel)
    return out

@@ -1,0 +1,83 @@
+import concourse.mybir as mybir
+
+F32, BF16, U16 = mybir.dt.float32, mybir.dt.bfloat16, mybir.dt.uint16
+ALU = mybir.AluOpType
+ABS = mybir.ActivationFunctionType.Abs
+
+P = 128
+C, S, N = 1024, 256, 128
+NB = C // P
+PREDICT_LINE = 0.6
+RELATION_GAP = 0.05
+
+FLOPS = 2 * 2 * C * C * N
+
+
+def tile_labelsmoothloss_kernel(tc, base, p, adj, prob, offs, out):
+    nc = tc.nc
+    p_blocks = p.rearrange("(b q) j -> q b j", q=P)
+    adj_blocks = adj.rearrange("(b q) c -> q b c", q=P)
+
+    with (
+        tc.tile_pool(name="held", bufs=1) as held,
+        tc.tile_pool(name="windows", bufs=NB) as windows,
+        tc.tile_pool(name="loads", bufs=NB) as loads,
+        tc.tile_pool(name="work", bufs=2) as work,
+        tc.psum_pool(name="sums", bufs=2) as sums,
+        tc.psum_pool(name="counts", bufs=1) as counts,
+    ):
+        offsets = held.tile([P, N // 16], U16, name="offsets")
+        nc.sync.dma_start(offsets[:], offs)
+
+        prior = held.tile([P, C], F32, name="prior")
+        nc.sync.dma_start(prior[:], prob.rearrange("c o -> (c o)").partition_broadcast(P))
+        p_sb = held.tile([P, NB, N], F32, name="p_sb")
+        nc.scalar.dma_start(p_sb[:], p_blocks)
+
+        conf = held.tile([P, NB, N], BF16, name="conf")
+        nc.vector.tensor_single_scalar(conf[:], p_sb[:], PREDICT_LINE, ALU.is_gt)
+        conf_p = held.tile([P, NB, N], BF16, name="conf_p")
+        nc.vector.scalar_tensor_tensor(conf_p[:], p_sb[:], PREDICT_LINE, p_sb[:], ALU.is_gt, ALU.mult)
+
+        ones = held.tile([P, P], BF16, name="ones")
+        nc.vector.memset(ones[:], 1.0)
+        count = counts.tile([P, N], F32, name="count")
+        for b in range(NB):
+            nc.tensor.matmul(count[:], ones[:], conf[:, b, :], start=(b == 0), stop=(b == NB - 1))
+
+        rel = held.tile([P, NB, N], F32, name="rel")
+        nc.vector.scalar_tensor_tensor(
+            rel[:], count[:].unsqueeze(1).to_broadcast([P, NB, N]), 1.0, conf[:], ALU.add, ALU.subtract
+        )
+        inv_rel = held.tile([P, NB, N], F32, name="inv_rel")
+        nc.vector.reciprocal(inv_rel[:], rel[:])
+
+        for cb in range(NB):
+            cols = slice(cb * P, (cb + 1) * P)
+            window = windows.tile([P, S], F32, name="window")
+            nc.scalar.dma_start(window[:], base[cols, :])
+            adj_c = loads.tile([P, NB, P], F32, name="adj_c")
+            nc.sync.dma_start(adj_c[:], adj_blocks[:, :, cols])
+
+            diff = work.tile([P, NB, P], BF16, name="diff")
+            nc.vector.tensor_tensor(
+                diff[:], adj_c[:], prior[:, cols].unsqueeze(1).to_broadcast([P, NB, P]), ALU.subtract
+            )
+            size = work.tile([P, NB, P], BF16, name="size")
+            nc.scalar.activation(size[:], diff[:], ABS)
+            dec = work.tile([P, NB, P], BF16, name="dec")
+            nc.vector.tensor_single_scalar(dec[:], diff[:], -RELATION_GAP, ALU.is_lt)
+            shifted = work.tile([P, NB, P], F32, name="shifted")
+            nc.vector.tensor_tensor(shifted[:], adj_c[:], dec[:], ALU.subtract)
+            w = work.tile([P, NB, P], BF16, name="w")
+            nc.vector.scalar_tensor_tensor(w[:], size[:], RELATION_GAP, shifted[:], ALU.is_gt, ALU.mult)
+
+            total = sums.tile([P, N], F32, name="total")
+            for b in range(NB):
+                nc.tensor.matmul(total[:], w[:, b, :], conf_p[:, b, :], start=(b == 0), stop=False)
+                nc.tensor.matmul(total[:], dec[:, b, :], conf[:, b, :], start=False, stop=(b == NB - 1))
+
+            num = work.tile([P, N], F32, name="num")
+            nc.vector.tensor_tensor(num[:], total[:], p_sb[:, cb, :], ALU.add)
+            nc.vector.tensor_tensor(window[:].indirect(offsets[:]), num[:], inv_rel[:, cb, :], ALU.mult)
+            nc.sync.dma_start(out[cols, :], window[:])

@@ -2,7 +2,7 @@ import concourse.mybir as mybir
 
 F32, BF16, U16 = mybir.dt.float32, mybir.dt.bfloat16, mybir.dt.uint16
 ALU = mybir.AluOpType
-ABS = mybir.ActivationFunctionType.Abs
+ABS, COPY = mybir.ActivationFunctionType.Abs, mybir.ActivationFunctionType.Copy
 
 P = 128
 C, S, N = 1024, 256, 128
@@ -38,6 +38,10 @@ def tile_labelsmoothloss_kernel(tc, base, p, adj, prob, offs, out):
         nc.vector.tensor_single_scalar(conf[:], p_sb[:], PREDICT_LINE, ALU.is_gt)
         conf_p = held.tile([P, NB, N], BF16, name="conf_p")
         nc.vector.scalar_tensor_tensor(conf_p[:], p_sb[:], PREDICT_LINE, p_sb[:], ALU.is_gt, ALU.mult)
+        rest = held.tile([P, NB, N], F32, name="rest")
+        nc.scalar.activation(rest[:], p_sb[:], COPY, bias=1.0, scale=-1.0)
+        conf_rest = held.tile([P, NB, N], BF16, name="conf_rest")
+        nc.vector.scalar_tensor_tensor(conf_rest[:], p_sb[:], PREDICT_LINE, rest[:], ALU.is_gt, ALU.mult)
 
         ones = held.tile([P, P], BF16, name="ones")
         nc.vector.memset(ones[:], 1.0)
@@ -67,15 +71,13 @@ def tile_labelsmoothloss_kernel(tc, base, p, adj, prob, offs, out):
             nc.scalar.activation(size[:], diff[:], ABS)
             dec = work.tile([P, NB, P], BF16, name="dec")
             nc.vector.tensor_single_scalar(dec[:], diff[:], -RELATION_GAP, ALU.is_lt)
-            shifted = work.tile([P, NB, P], F32, name="shifted")
-            nc.vector.tensor_tensor(shifted[:], adj_c[:], dec[:], ALU.subtract)
-            w = work.tile([P, NB, P], BF16, name="w")
-            nc.vector.scalar_tensor_tensor(w[:], size[:], RELATION_GAP, shifted[:], ALU.is_gt, ALU.mult)
+            hit_adj = work.tile([P, NB, P], BF16, name="hit_adj")
+            nc.vector.scalar_tensor_tensor(hit_adj[:], size[:], RELATION_GAP, adj_c[:], ALU.is_gt, ALU.mult)
 
             total = sums.tile([P, N], F32, name="total")
             for b in range(NB):
-                nc.tensor.matmul(total[:], w[:, b, :], conf_p[:, b, :], start=(b == 0), stop=False)
-                nc.tensor.matmul(total[:], dec[:, b, :], conf[:, b, :], start=False, stop=(b == NB - 1))
+                nc.tensor.matmul(total[:], hit_adj[:, b, :], conf_p[:, b, :], start=(b == 0), stop=False)
+                nc.tensor.matmul(total[:], dec[:, b, :], conf_rest[:, b, :], start=False, stop=(b == NB - 1))
 
             num = work.tile([P, N], F32, name="num")
             nc.vector.tensor_tensor(num[:], total[:], p_sb[:, cb, :], ALU.add)

@@ -1,4 +1,5 @@
 import concourse.mybir as mybir
+from concourse.masks import make_identity
 
 F32, BF16, U16 = mybir.dt.float32, mybir.dt.bfloat16, mybir.dt.uint16
 ALU = mybir.AluOpType
@@ -20,19 +21,30 @@ def tile_labelsmoothloss_kernel(tc, base, p, adj, prob, offs, out):
 
     with (
         tc.tile_pool(name="held", bufs=1) as held,
-        tc.tile_pool(name="windows", bufs=NB) as windows,
         tc.tile_pool(name="loads", bufs=NB) as loads,
-        tc.tile_pool(name="work", bufs=2) as work,
-        tc.psum_pool(name="sums", bufs=2) as sums,
+        tc.tile_pool(name="work", bufs=3) as work,
+        tc.psum_pool(name="sums", bufs=3) as sums,
         tc.psum_pool(name="counts", bufs=1) as counts,
     ):
         offsets = held.tile([P, N // 16], U16, name="offsets")
         nc.sync.dma_start(offsets[:], offs)
-
+        p_sb = held.tile([P, NB, N], F32, name="p_sb")
+        nc.sync.dma_start(p_sb[:], p_blocks)
         prior = held.tile([P, C], F32, name="prior")
         nc.sync.dma_start(prior[:], prob.rearrange("c o -> (c o)").partition_broadcast(P))
-        p_sb = held.tile([P, NB, N], F32, name="p_sb")
-        nc.scalar.dma_start(p_sb[:], p_blocks)
+        adj_pieces, windows = [], []
+        for cb in range(NB):
+            adj_c = loads.tile([P, NB, P], F32, name="adj_c")
+            nc.sync.dma_start(adj_c[:], adj_blocks[:, :, cb * P : (cb + 1) * P])
+            adj_pieces.append(adj_c)
+            window = loads.tile([P, S], F32, name="window")
+            nc.sync.dma_start(window[:], base[cb * P : (cb + 1) * P, :])
+            windows.append(window)
+
+        ones = held.tile([P, P], BF16, name="ones")
+        nc.vector.memset(ones[:], 1.0)
+        identity = held.tile([P, P], F32, name="identity")
+        make_identity(nc, identity[:])
 
         conf = held.tile([P, NB, N], BF16, name="conf")
         nc.vector.tensor_single_scalar(conf[:], p_sb[:], PREDICT_LINE, ALU.is_gt)
@@ -43,43 +55,64 @@ def tile_labelsmoothloss_kernel(tc, base, p, adj, prob, offs, out):
         conf_rest = held.tile([P, NB, N], BF16, name="conf_rest")
         nc.vector.scalar_tensor_tensor(conf_rest[:], p_sb[:], PREDICT_LINE, rest[:], ALU.is_gt, ALU.mult)
 
-        ones = held.tile([P, P], BF16, name="ones")
-        nc.vector.memset(ones[:], 1.0)
         count = counts.tile([P, N], F32, name="count")
         for b in range(NB):
             nc.tensor.matmul(count[:], ones[:], conf[:, b, :], start=(b == 0), stop=(b == NB - 1))
 
-        rel = held.tile([P, NB, N], F32, name="rel")
-        nc.vector.scalar_tensor_tensor(
-            rel[:], count[:].unsqueeze(1).to_broadcast([P, NB, N]), 1.0, conf[:], ALU.add, ALU.subtract
-        )
         inv_rel = held.tile([P, NB, N], F32, name="inv_rel")
-        nc.vector.reciprocal(inv_rel[:], rel[:])
 
-        for cb in range(NB):
-            cols = slice(cb * P, (cb + 1) * P)
-            window = windows.tile([P, S], F32, name="window")
-            nc.scalar.dma_start(window[:], base[cols, :])
-            adj_c = loads.tile([P, NB, P], F32, name="adj_c")
-            nc.sync.dma_start(adj_c[:], adj_blocks[:, :, cols])
+        def invert_rel():
+            den = held.tile([P, 2, N], F32, name="den")
+            nc.vector.tensor_scalar_add(den[:, 0, :], count[:], 1.0)
+            nc.vector.tensor_scalar_max(den[:, 1, :], count[:], 1.0)
+            inv = held.tile([P, 2, N], F32, name="inv")
+            nc.vector.reciprocal(inv[:], den[:])
+            raise_own = held.tile([P, NB, N], F32, name="raise_own")
+            nc.vector.tensor_tensor(
+                raise_own[:], conf[:], inv[:, 1, :].unsqueeze(1).to_broadcast([P, NB, N]), ALU.mult
+            )
+            nc.vector.scalar_tensor_tensor(
+                inv_rel[:], raise_own[:], 1.0, inv[:, 0, :].unsqueeze(1).to_broadcast([P, NB, N]), ALU.add, ALU.mult
+            )
 
+        sizes, decs, nums = {}, {}, {}
+
+        def classify(cb):
             diff = work.tile([P, NB, P], BF16, name="diff")
             nc.vector.tensor_tensor(
-                diff[:], adj_c[:], prior[:, cols].unsqueeze(1).to_broadcast([P, NB, P]), ALU.subtract
+                diff[:],
+                adj_pieces[cb][:],
+                prior[:, cb * P : (cb + 1) * P].unsqueeze(1).to_broadcast([P, NB, P]),
+                ALU.subtract,
             )
-            size = work.tile([P, NB, P], BF16, name="size")
-            nc.scalar.activation(size[:], diff[:], ABS)
-            dec = work.tile([P, NB, P], BF16, name="dec")
-            nc.vector.tensor_single_scalar(dec[:], diff[:], -RELATION_GAP, ALU.is_lt)
+            sizes[cb] = work.tile([P, NB, P], BF16, name="size")
+            nc.scalar.activation(sizes[cb][:], diff[:], ABS)
+            decs[cb] = work.tile([P, NB, P], BF16, name="dec")
+            nc.vector.tensor_single_scalar(decs[cb][:], diff[:], -RELATION_GAP, ALU.is_lt)
+
+        def weigh(cb):
             hit_adj = work.tile([P, NB, P], BF16, name="hit_adj")
-            nc.vector.scalar_tensor_tensor(hit_adj[:], size[:], RELATION_GAP, adj_c[:], ALU.is_gt, ALU.mult)
-
-            total = sums.tile([P, N], F32, name="total")
+            nc.vector.scalar_tensor_tensor(
+                hit_adj[:], sizes[cb][:], RELATION_GAP, adj_pieces[cb][:], ALU.is_gt, ALU.mult
+            )
+            num_ps = sums.tile([P, N], F32, name="num_ps")
+            nc.tensor.matmul(num_ps[:], identity[:], p_sb[:, cb, :], start=True, stop=False)
             for b in range(NB):
-                nc.tensor.matmul(total[:], hit_adj[:, b, :], conf_p[:, b, :], start=(b == 0), stop=False)
-                nc.tensor.matmul(total[:], dec[:, b, :], conf_rest[:, b, :], start=False, stop=(b == NB - 1))
+                nc.tensor.matmul(num_ps[:], hit_adj[:, b, :], conf_p[:, b, :], start=False, stop=False)
+                nc.tensor.matmul(num_ps[:], decs[cb][:, b, :], conf_rest[:, b, :], start=False, stop=(b == NB - 1))
+            nums[cb] = work.tile([P, N], F32, name="num")
+            nc.scalar.copy(nums[cb][:], num_ps[:])
 
-            num = work.tile([P, N], F32, name="num")
-            nc.vector.tensor_tensor(num[:], total[:], p_sb[:, cb, :], ALU.add)
-            nc.vector.tensor_tensor(window[:].indirect(offsets[:]), num[:], inv_rel[:, cb, :], ALU.mult)
-            nc.sync.dma_start(out[cols, :], window[:])
+        def place(cb):
+            nc.vector.tensor_tensor(windows[cb][:].indirect(offsets[:]), nums[cb][:], inv_rel[:, cb, :], ALU.mult)
+            nc.sync.dma_start(out[cb * P : (cb + 1) * P, :], windows[cb][:])
+
+        for step in range(NB + 2):
+            if step < NB:
+                classify(step)
+            if step == 1:
+                invert_rel()
+            if 1 <= step <= NB:
+                weigh(step - 1)
+            if step >= 2:
+                place(step - 2)

@@ -3,13 +3,18 @@ from concourse.masks import make_identity
 
 F32, BF16, U16 = mybir.dt.float32, mybir.dt.bfloat16, mybir.dt.uint16
 ALU = mybir.AluOpType
-ABS, COPY = mybir.ActivationFunctionType.Abs, mybir.ActivationFunctionType.Copy
+ACT = mybir.ActivationFunctionType
+ABS, COPY, IDENTITY, SIGMOID = ACT.Abs, ACT.Copy, ACT.Identity, ACT.Sigmoid
 
 P = 128
 C, S, N = 1024, 256, 128
 NB = C // P
+BANK = 512 // P
 PREDICT_LINE = 0.6
 RELATION_GAP = 0.05
+STEEP = 4096.0
+WEIGH_AFTER = 2
+PLACE_AFTER = 3
 
 FLOPS = 2 * 2 * C * C * N
 
@@ -18,77 +23,46 @@ def tile_labelsmoothloss_kernel(tc, base, p, adj, prob, offs, out):
     nc = tc.nc
     p_blocks = p.rearrange("(b q) j -> q b j", q=P)
     adj_blocks = adj.rearrange("(b q) c -> q b c", q=P)
+    prior_row = prob.rearrange("c o -> (c o)")
 
     with (
         tc.tile_pool(name="held", bufs=1) as held,
         tc.tile_pool(name="loads", bufs=NB) as loads,
-        tc.tile_pool(name="work", bufs=3) as work,
+        tc.tile_pool(name="work", bufs=WEIGH_AFTER + PLACE_AFTER) as work,
         tc.psum_pool(name="sums", bufs=3) as sums,
-        tc.psum_pool(name="counts", bufs=1) as counts,
+        tc.psum_pool(name="flips", bufs=2) as flips,
     ):
         offsets = held.tile([P, N // 16], U16, name="offsets")
         nc.sync.dma_start(offsets[:], offs)
         p_sb = held.tile([P, NB, N], F32, name="p_sb")
         nc.sync.dma_start(p_sb[:], p_blocks)
-        prior = held.tile([P, C], F32, name="prior")
-        nc.sync.dma_start(prior[:], prob.rearrange("c o -> (c o)").partition_broadcast(P))
-        adj_pieces, windows = [], []
+        priors, adj_pieces, windows = [], [], []
         for cb in range(NB):
+            block = slice(cb * P, (cb + 1) * P)
+            prior = loads.tile([P, P], F32, name="prior")
+            nc.sync.dma_start(prior[:], prior_row[block].partition_broadcast(P))
+            priors.append(prior)
             adj_c = loads.tile([P, NB, P], F32, name="adj_c")
-            nc.sync.dma_start(adj_c[:], adj_blocks[:, :, cb * P : (cb + 1) * P])
+            nc.sync.dma_start(adj_c[:], adj_blocks[:, :, block])
             adj_pieces.append(adj_c)
             window = loads.tile([P, S], F32, name="window")
-            nc.sync.dma_start(window[:], base[cb * P : (cb + 1) * P, :])
+            nc.sync.dma_start(window[:], base[block, :])
             windows.append(window)
 
-        ones = held.tile([P, P], BF16, name="ones")
-        nc.vector.memset(ones[:], 1.0)
         identity = held.tile([P, P], F32, name="identity")
         make_identity(nc, identity[:])
-
-        conf = held.tile([P, NB, N], BF16, name="conf")
-        nc.vector.tensor_single_scalar(conf[:], p_sb[:], PREDICT_LINE, ALU.is_gt)
-        conf_p = held.tile([P, NB, N], BF16, name="conf_p")
-        nc.vector.scalar_tensor_tensor(conf_p[:], p_sb[:], PREDICT_LINE, p_sb[:], ALU.is_gt, ALU.mult)
-        rest = held.tile([P, NB, N], F32, name="rest")
-        nc.scalar.activation(rest[:], p_sb[:], COPY, bias=1.0, scale=-1.0)
-        conf_rest = held.tile([P, NB, N], BF16, name="conf_rest")
-        nc.vector.scalar_tensor_tensor(conf_rest[:], p_sb[:], PREDICT_LINE, rest[:], ALU.is_gt, ALU.mult)
-
-        count = counts.tile([P, N], F32, name="count")
-        for b in range(NB):
-            nc.tensor.matmul(count[:], ones[:], conf[:, b, :], start=(b == 0), stop=(b == NB - 1))
-
-        inv_rel = held.tile([P, NB, N], F32, name="inv_rel")
-
-        def invert_rel():
-            den = held.tile([P, 2, N], F32, name="den")
-            nc.vector.tensor_scalar_add(den[:, 0, :], count[:], 1.0)
-            nc.vector.tensor_scalar_max(den[:, 1, :], count[:], 1.0)
-            inv = held.tile([P, 2, N], F32, name="inv")
-            nc.vector.reciprocal(inv[:], den[:])
-            raise_own = held.tile([P, NB, N], F32, name="raise_own")
-            nc.vector.tensor_tensor(
-                raise_own[:], conf[:], inv[:, 1, :].unsqueeze(1).to_broadcast([P, NB, N]), ALU.mult
-            )
-            nc.vector.scalar_tensor_tensor(
-                inv_rel[:], raise_own[:], 1.0, inv[:, 0, :].unsqueeze(1).to_broadcast([P, NB, N]), ALU.add, ALU.mult
-            )
 
         sizes, decs, nums = {}, {}, {}
 
         def classify(cb):
             diff = work.tile([P, NB, P], BF16, name="diff")
             nc.vector.tensor_tensor(
-                diff[:],
-                adj_pieces[cb][:],
-                prior[:, cb * P : (cb + 1) * P].unsqueeze(1).to_broadcast([P, NB, P]),
-                ALU.subtract,
+                diff[:], adj_pieces[cb][:], priors[cb][:].unsqueeze(1).to_broadcast([P, NB, P]), ALU.subtract
             )
             sizes[cb] = work.tile([P, NB, P], BF16, name="size")
             nc.scalar.activation(sizes[cb][:], diff[:], ABS)
             decs[cb] = work.tile([P, NB, P], BF16, name="dec")
-            nc.vector.tensor_single_scalar(decs[cb][:], diff[:], -RELATION_GAP, ALU.is_lt)
+            nc.scalar.activation(decs[cb][:], diff[:], SIGMOID, bias=-STEEP * RELATION_GAP, scale=-STEEP)
 
         def weigh(cb):
             hit_adj = work.tile([P, NB, P], BF16, name="hit_adj")
@@ -107,12 +81,54 @@ def tile_labelsmoothloss_kernel(tc, base, p, adj, prob, offs, out):
             nc.vector.tensor_tensor(windows[cb][:].indirect(offsets[:]), nums[cb][:], inv_rel[:, cb, :], ALU.mult)
             nc.sync.dma_start(out[cb * P : (cb + 1) * P, :], windows[cb][:])
 
-        for step in range(NB + 2):
+
+        conf_p = held.tile([P, NB, N], BF16, name="conf_p")
+        nc.vector.scalar_tensor_tensor(conf_p[:], p_sb[:], PREDICT_LINE, p_sb[:], ALU.is_gt, ALU.mult)
+        rest = held.tile([P, NB, N], F32, name="rest")
+        nc.scalar.activation(rest[:], p_sb[:], COPY, bias=1.0, scale=-1.0)
+
+        conf_t = held.tile([P, NB, P], F32, name="conf_t")
+        half_counts = held.tile([P, NB // BANK], F32, name="half_counts")
+        for h in range(NB // BANK):
+            p_t = flips.tile([P, BANK, P], F32, name="p_t")
+            for i in range(BANK):
+                nc.tensor.transpose(p_t[:, i, :], p_sb[:, h * BANK + i, :], identity[:])
+            nc.scalar.activation(
+                conf_t[:, h * BANK : (h + 1) * BANK, :],
+                p_t[:],
+                SIGMOID,
+                bias=-STEEP * PREDICT_LINE,
+                scale=STEEP,
+                accum_out=half_counts[:, h : h + 1],
+            )
+
+        classify(0)
+
+        conf_rest = held.tile([P, NB, N], BF16, name="conf_rest")
+        nc.vector.scalar_tensor_tensor(conf_rest[:], p_sb[:], PREDICT_LINE, rest[:], ALU.is_gt, ALU.mult)
+
+        classify(1)
+
+        den = held.tile([P, 2], F32, name="den")
+        nc.vector.tensor_scalar(den[:, 0:1], half_counts[:, 0:1], half_counts[:, 1:2], 1.0, ALU.add, ALU.add)
+        nc.vector.tensor_scalar(den[:, 1:2], half_counts[:, 0:1], half_counts[:, 1:2], 1.0, ALU.add, ALU.max)
+        inv = held.tile([P, 2], F32, name="inv")
+        nc.vector.reciprocal(inv[:], den[:])
+        slope = held.tile([P, 1], F32, name="slope")
+        nc.vector.tensor_tensor(slope[:], inv[:, 0:1], inv[:, 1:2], ALU.mult)
+        inv_rel_t = held.tile([P, NB, P], F32, name="inv_rel_t")
+        nc.vector.tensor_scalar(inv_rel_t[:], conf_t[:], slope[:, 0:1], inv[:, 0:1], ALU.mult, ALU.add)
+        inv_rel = held.tile([P, NB, N], F32, name="inv_rel")
+        for h in range(NB // BANK):
+            back = flips.tile([P, BANK, N], F32, name="back")
+            for i in range(BANK):
+                nc.tensor.transpose(back[:, i, :], inv_rel_t[:, h * BANK + i, :], identity[:])
+            nc.scalar.copy(inv_rel[:, h * BANK : (h + 1) * BANK, :], back[:])
+
+        for step in range(2, NB + WEIGH_AFTER + PLACE_AFTER):
             if step < NB:
                 classify(step)
-            if step == 1:
-                invert_rel()
-            if 1 <= step <= NB:
-                weigh(step - 1)
-            if step >= 2:
-                place(step - 2)
+            if step - WEIGH_AFTER < NB:
+                weigh(step - WEIGH_AFTER)
+            if step >= WEIGH_AFTER + PLACE_AFTER:
+                place(step - WEIGH_AFTER - PLACE_AFTER)

@@ -29,7 +29,7 @@ def tile_labelsmoothloss_kernel(tc, base, p, adj, prob, offs, out):
         tc.tile_pool(name="held", bufs=1) as held,
         tc.tile_pool(name="loads", bufs=NB) as loads,
         tc.tile_pool(name="work", bufs=WEIGH_AFTER + PLACE_AFTER) as work,
-        tc.psum_pool(name="sums", bufs=3) as sums,
+        tc.psum_pool(name="sums", bufs=PLACE_AFTER + 1) as sums,
         tc.psum_pool(name="flips", bufs=2) as flips,
     ):
         offsets = held.tile([P, N // 16], U16, name="offsets")
@@ -51,8 +51,11 @@ def tile_labelsmoothloss_kernel(tc, base, p, adj, prob, offs, out):
 
         identity = held.tile([P, P], F32, name="identity")
         make_identity(nc, identity[:])
+        scratch = held.tile([P, 1], F32, name="scratch")
+        nc.vector.memset(scratch[:], 0.0)
+        nc.scalar.activation(scratch[:], scratch[:], SIGMOID)
 
-        sizes, decs, nums = {}, {}, {}
+        sizes, decs, sums_over_k = {}, {}, {}
 
         def classify(cb):
             diff = work.tile([P, NB, P], BF16, name="diff")
@@ -69,16 +72,16 @@ def tile_labelsmoothloss_kernel(tc, base, p, adj, prob, offs, out):
             nc.vector.scalar_tensor_tensor(
                 hit_adj[:], sizes[cb][:], RELATION_GAP, adj_pieces[cb][:], ALU.is_gt, ALU.mult
             )
-            num_ps = sums.tile([P, N], F32, name="num_ps")
-            nc.tensor.matmul(num_ps[:], identity[:], p_sb[:, cb, :], start=True, stop=False)
+            both = sums.tile([P, N], F32, name="both")
             for b in range(NB):
-                nc.tensor.matmul(num_ps[:], hit_adj[:, b, :], conf_p[:, b, :], start=False, stop=False)
-                nc.tensor.matmul(num_ps[:], decs[cb][:, b, :], conf_rest[:, b, :], start=False, stop=(b == NB - 1))
-            nums[cb] = work.tile([P, N], F32, name="num")
-            nc.scalar.copy(nums[cb][:], num_ps[:])
+                nc.tensor.matmul(both[:], hit_adj[:, b, :], conf_p[:, b, :], start=(b == 0), stop=False)
+                nc.tensor.matmul(both[:], decs[cb][:, b, :], conf_rest[:, b, :], start=False, stop=(b == NB - 1))
+            sums_over_k[cb] = both
 
         def place(cb):
-            nc.vector.tensor_tensor(windows[cb][:].indirect(offsets[:]), nums[cb][:], inv_rel[:, cb, :], ALU.mult)
+            num = work.tile([P, N], F32, name="num")
+            nc.vector.tensor_tensor(num[:], sums_over_k[cb][:], p_sb[:, cb, :], ALU.add)
+            nc.vector.tensor_tensor(windows[cb][:].indirect(offsets[:]), num[:], inv_rel[:, cb, :], ALU.mult)
             nc.sync.dma_start(out[cb * P : (cb + 1) * P, :], windows[cb][:])
 
 
@@ -90,7 +93,7 @@ def tile_labelsmoothloss_kernel(tc, base, p, adj, prob, offs, out):
         conf_t = held.tile([P, NB, P], F32, name="conf_t")
         half_counts = held.tile([P, NB // BANK], F32, name="half_counts")
         for h in range(NB // BANK):
-            p_t = flips.tile([P, BANK, P], F32, name="p_t")
+            p_t = flips.tile([P, BANK, P], F32, name="p_t", tag="flip")
             for i in range(BANK):
                 nc.tensor.transpose(p_t[:, i, :], p_sb[:, h * BANK + i, :], identity[:])
             nc.scalar.activation(
@@ -120,7 +123,7 @@ def tile_labelsmoothloss_kernel(tc, base, p, adj, prob, offs, out):
         nc.vector.tensor_scalar(inv_rel_t[:], conf_t[:], slope[:, 0:1], inv[:, 0:1], ALU.mult, ALU.add)
         inv_rel = held.tile([P, NB, N], F32, name="inv_rel")
         for h in range(NB // BANK):
-            back = flips.tile([P, BANK, N], F32, name="back")
+            back = flips.tile([P, BANK, N], F32, name="back", tag="flip")
             for i in range(BANK):
                 nc.tensor.transpose(back[:, i, :], inv_rel_t[:, h * BANK + i, :], identity[:])
             nc.scalar.copy(inv_rel[:, h * BANK : (h + 1) * BANK, :], back[:])

@@ -10,11 +10,15 @@ P = 128
 C, S, N = 1024, 256, 128
 NB = C // P
 BANK = 512 // P
+W = 256
+GROUP = W // P
+DEPTH = C // W
+PIECES = NB // DEPTH
 PREDICT_LINE = 0.6
 RELATION_GAP = 0.05
 STEEP = 4096.0
 WEIGH_AFTER = 2
-PLACE_AFTER = 3
+PLACE_FROM = 6
 
 FLOPS = 2 * 2 * C * C * N
 
@@ -28,8 +32,8 @@ def tile_labelsmoothloss_kernel(tc, base, p, adj, prob, offs, out):
     with (
         tc.tile_pool(name="held", bufs=1) as held,
         tc.tile_pool(name="loads", bufs=NB) as loads,
-        tc.tile_pool(name="work", bufs=WEIGH_AFTER + PLACE_AFTER) as work,
-        tc.psum_pool(name="sums", bufs=PLACE_AFTER + 1) as sums,
+        tc.tile_pool(name="work", bufs=6) as work,
+        tc.psum_pool(name="sums", bufs=2 * GROUP) as sums,
         tc.psum_pool(name="flips", bufs=2) as flips,
     ):
         offsets = held.tile([P, N // 16], U16, name="offsets")
@@ -37,17 +41,18 @@ def tile_labelsmoothloss_kernel(tc, base, p, adj, prob, offs, out):
         p_sb = held.tile([P, NB, N], F32, name="p_sb")
         nc.sync.dma_start(p_sb[:], p_blocks)
         priors, adj_pieces, windows = [], [], []
-        for cb in range(NB):
-            block = slice(cb * P, (cb + 1) * P)
-            prior = loads.tile([P, P], F32, name="prior")
-            nc.sync.dma_start(prior[:], prior_row[block].partition_broadcast(P))
+        for g in range(C // W):
+            prior = loads.tile([P, W], F32, name="prior")
+            nc.sync.dma_start(prior[:], prior_row[g * W : (g + 1) * W].partition_broadcast(P))
             priors.append(prior)
-            adj_c = loads.tile([P, NB, P], F32, name="adj_c")
-            nc.sync.dma_start(adj_c[:], adj_blocks[:, :, block])
-            adj_pieces.append(adj_c)
-            window = loads.tile([P, S], F32, name="window")
-            nc.sync.dma_start(window[:], base[block, :])
-            windows.append(window)
+            for i in range(PIECES):
+                adj_c = loads.tile([P, DEPTH, W], F32, name="adj_c")
+                nc.sync.dma_start(adj_c[:], adj_blocks[:, i * DEPTH : (i + 1) * DEPTH, g * W : (g + 1) * W])
+                adj_pieces.append(adj_c)
+            for n in range(g * GROUP, (g + 1) * GROUP):
+                window = loads.tile([P, S], F32, name="window")
+                nc.sync.dma_start(window[:], base[n * P : (n + 1) * P, :])
+                windows.append(window)
 
         identity = held.tile([P, P], F32, name="identity")
         make_identity(nc, identity[:])
@@ -55,34 +60,45 @@ def tile_labelsmoothloss_kernel(tc, base, p, adj, prob, offs, out):
         nc.vector.memset(scratch[:], 0.0)
         nc.scalar.activation(scratch[:], scratch[:], SIGMOID)
 
-        sizes, decs, sums_over_k = {}, {}, {}
+        sizes, decs, nums_ps, nums = {}, {}, {}, {}
 
-        def classify(cb):
-            diff = work.tile([P, NB, P], BF16, name="diff")
+        def classify(t):
+            diff = work.tile([P, DEPTH, W], BF16, name="diff")
             nc.vector.tensor_tensor(
-                diff[:], adj_pieces[cb][:], priors[cb][:].unsqueeze(1).to_broadcast([P, NB, P]), ALU.subtract
+                diff[:], adj_pieces[t][:], priors[t // PIECES][:].unsqueeze(1).to_broadcast([P, DEPTH, W]), ALU.subtract
             )
-            sizes[cb] = work.tile([P, NB, P], BF16, name="size")
-            nc.scalar.activation(sizes[cb][:], diff[:], ABS)
-            decs[cb] = work.tile([P, NB, P], BF16, name="dec")
-            nc.scalar.activation(decs[cb][:], diff[:], SIGMOID, bias=-STEEP * RELATION_GAP, scale=-STEEP)
+            sizes[t] = work.tile([P, DEPTH, W], BF16, name="size")
+            nc.scalar.activation(sizes[t][:], diff[:], ABS)
+            decs[t] = work.tile([P, DEPTH, W], BF16, name="dec")
+            nc.scalar.activation(decs[t][:], diff[:], SIGMOID, bias=-STEEP * RELATION_GAP, scale=-STEEP)
 
-        def weigh(cb):
-            hit_adj = work.tile([P, NB, P], BF16, name="hit_adj")
-            nc.vector.scalar_tensor_tensor(
-                hit_adj[:], sizes[cb][:], RELATION_GAP, adj_pieces[cb][:], ALU.is_gt, ALU.mult
-            )
-            both = sums.tile([P, N], F32, name="both")
-            for b in range(NB):
-                nc.tensor.matmul(both[:], hit_adj[:, b, :], conf_p[:, b, :], start=(b == 0), stop=False)
-                nc.tensor.matmul(both[:], decs[cb][:, b, :], conf_rest[:, b, :], start=False, stop=(b == NB - 1))
-            sums_over_k[cb] = both
+        def weigh(t):
+            hit_adj = work.tile([P, DEPTH, W], BF16, name="hit_adj")
+            nc.vector.scalar_tensor_tensor(hit_adj[:], sizes[t][:], RELATION_GAP, adj_pieces[t][:], ALU.is_gt, ALU.mult)
+            g, i = divmod(t, PIECES)
+            for m in range(GROUP):
+                n = g * GROUP + m
+                if i == 0:
+                    nums_ps[n] = sums.tile([P, N], F32, name="num_ps")
+                    nc.tensor.matmul(nums_ps[n][:], identity[:], p_sb[:, n, :], start=True, stop=False)
+                for b in range(DEPTH):
+                    k = i * DEPTH + b
+                    last = i == PIECES - 1 and b == DEPTH - 1
+                    nc.tensor.matmul(
+                        nums_ps[n][:], hit_adj[:, b, m * P : (m + 1) * P], conf_p[:, k, :], start=False, stop=False
+                    )
+                    nc.tensor.matmul(
+                        nums_ps[n][:], decs[t][:, b, m * P : (m + 1) * P], conf_rest[:, k, :], start=False, stop=last
+                    )
 
-        def place(cb):
-            num = work.tile([P, N], F32, name="num")
-            nc.vector.tensor_tensor(num[:], sums_over_k[cb][:], p_sb[:, cb, :], ALU.add)
-            nc.vector.tensor_tensor(windows[cb][:].indirect(offsets[:]), num[:], inv_rel[:, cb, :], ALU.mult)
-            nc.sync.dma_start(out[cb * P : (cb + 1) * P, :], windows[cb][:])
+        def collect(g):
+            for n in range(g * GROUP, (g + 1) * GROUP):
+                nums[n] = work.tile([P, N], F32, name="num")
+                nc.scalar.copy(nums[n][:], nums_ps[n][:])
+
+        def place(n):
+            nc.vector.tensor_tensor(windows[n][:].indirect(offsets[:]), nums[n][:], inv_rel[:, n, :], ALU.mult)
+            nc.sync.dma_start(out[n * P : (n + 1) * P, :], windows[n][:])
 
 
         conf_p = held.tile([P, NB, N], BF16, name="conf_p")
@@ -128,10 +144,13 @@ def tile_labelsmoothloss_kernel(tc, base, p, adj, prob, offs, out):
                 nc.tensor.transpose(back[:, i, :], inv_rel_t[:, h * BANK + i, :], identity[:])
             nc.scalar.copy(inv_rel[:, h * BANK : (h + 1) * BANK, :], back[:])
 
-        for step in range(2, NB + WEIGH_AFTER + PLACE_AFTER):
+        for step in range(2, NB + PLACE_FROM):
             if step < NB:
                 classify(step)
+            weighed = step - WEIGH_AFTER - 1
+            if weighed >= 0 and weighed < NB and weighed % PIECES == PIECES - 1:
+                collect(weighed // PIECES)
             if step - WEIGH_AFTER < NB:
                 weigh(step - WEIGH_AFTER)
-            if step >= WEIGH_AFTER + PLACE_AFTER:
-                place(step - WEIGH_AFTER - PLACE_AFTER)
+            if step >= PLACE_FROM:
+                place(step - PLACE_FROM)

@@ -49,10 +49,10 @@ def tile_labelsmoothloss_kernel(tc, base, p, adj, prob, offs, out):
                 adj_c = loads.tile([P, DEPTH, W], F32, name="adj_c")
                 nc.sync.dma_start(adj_c[:], adj_blocks[:, i * DEPTH : (i + 1) * DEPTH, g * W : (g + 1) * W])
                 adj_pieces.append(adj_c)
-            for n in range(g * GROUP, (g + 1) * GROUP):
-                window = loads.tile([P, S], F32, name="window")
-                nc.sync.dma_start(window[:], base[n * P : (n + 1) * P, :])
-                windows.append(window)
+        for n in range(NB):
+            window = loads.tile([P, S], F32, name="window")
+            nc.sync.dma_start(window[:], base[n * P : (n + 1) * P, :])
+            windows.append(window)
 
         identity = held.tile([P, P], F32, name="identity")
         make_identity(nc, identity[:])

@@ -70,7 +70,10 @@ def tile_labelsmoothloss_kernel(tc, base, p, adj, prob, offs, out):
             sizes[t] = work.tile([P, DEPTH, W], BF16, name="size")
             nc.scalar.activation(sizes[t][:], diff[:], ABS)
             decs[t] = work.tile([P, DEPTH, W], BF16, name="dec")
-            nc.scalar.activation(decs[t][:], diff[:], SIGMOID, bias=-STEEP * RELATION_GAP, scale=-STEEP)
+            if t % 4 == 2:
+                nc.vector.tensor_single_scalar(decs[t][:], diff[:], -RELATION_GAP, ALU.is_lt)
+            else:
+                nc.scalar.activation(decs[t][:], diff[:], SIGMOID, bias=-STEEP * RELATION_GAP, scale=-STEEP)
 
         def weigh(t):
             hit_adj = work.tile([P, DEPTH, W], BF16, name="hit_adj")

@@ -1,10 +1,10 @@
 import concourse.mybir as mybir
 from concourse.masks import make_identity
 
-F32, BF16, U16 = mybir.dt.float32, mybir.dt.bfloat16, mybir.dt.uint16
+F32, BF16, U16, I32 = mybir.dt.float32, mybir.dt.bfloat16, mybir.dt.uint16, mybir.dt.int32
 ALU = mybir.AluOpType
 ACT = mybir.ActivationFunctionType
-ABS, COPY, IDENTITY, SIGMOID = ACT.Abs, ACT.Copy, ACT.Identity, ACT.Sigmoid
+SIGMOID = ACT.Sigmoid
 
 P = 128
 C, S, N = 1024, 256, 128
@@ -17,7 +17,7 @@ PIECES = NB // DEPTH
 PREDICT_LINE = 0.6
 RELATION_GAP = 0.05
 STEEP = 4096.0
-WEIGH_AFTER = 2
+NO_SIGNS = 0x7FFF7FFF
 PLACE_FROM = 6
 
 FLOPS = 2 * 2 * C * C * N
@@ -60,24 +60,36 @@ def tile_labelsmoothloss_kernel(tc, base, p, adj, prob, offs, out):
         nc.vector.memset(scratch[:], 0.0)
         nc.scalar.activation(scratch[:], scratch[:], SIGMOID)
 
-        sizes, decs, nums_ps, nums = {}, {}, {}, {}
+        priors_bf, adj_bfs, diffs, sizes, decs, hits, nums_ps, nums = {}, {}, {}, {}, {}, {}, {}, {}
 
-        def classify(t):
-            diff = work.tile([P, DEPTH, W], BF16, name="diff")
+        def round_off(t):
+            if t % PIECES == 0:
+                priors_bf[t // PIECES] = work.tile([P, W], BF16, name="prior_bf")
+                nc.vector.tensor_copy(priors_bf[t // PIECES][:], priors[t // PIECES][:])
+            adj_bfs[t] = work.tile([P, DEPTH, W], BF16, name="adj_bf")
+            nc.scalar.copy(adj_bfs[t][:], adj_pieces[t][:])
+
+        def subtract(t):
+            diffs[t] = work.tile([P, DEPTH, W], BF16, name="diff")
             nc.vector.tensor_tensor(
-                diff[:], adj_pieces[t][:], priors[t // PIECES][:].unsqueeze(1).to_broadcast([P, DEPTH, W]), ALU.subtract
+                diffs[t][:], adj_bfs[t][:], priors_bf[t // PIECES][:].unsqueeze(1).to_broadcast([P, DEPTH, W]), ALU.subtract
             )
+
+        def measure(t):
             sizes[t] = work.tile([P, DEPTH, W], BF16, name="size")
-            nc.scalar.activation(sizes[t][:], diff[:], ABS)
+            nc.vector.tensor_single_scalar(sizes[t][:].bitcast(I32), diffs[t][:].bitcast(I32), NO_SIGNS, ALU.bitwise_and)
+
+        def find_dec(t):
             decs[t] = work.tile([P, DEPTH, W], BF16, name="dec")
-            if t % 4 == 2:
-                nc.vector.tensor_single_scalar(decs[t][:], diff[:], -RELATION_GAP, ALU.is_lt)
-            else:
-                nc.scalar.activation(decs[t][:], diff[:], SIGMOID, bias=-STEEP * RELATION_GAP, scale=-STEEP)
+            nc.vector.tensor_single_scalar(decs[t][:], diffs[t][:], -RELATION_GAP, ALU.is_lt)
+
+        def find_hit(t):
+            hits[t] = work.tile([P, DEPTH, W], BF16, name="hit")
+            nc.vector.tensor_single_scalar(hits[t][:], sizes[t][:], RELATION_GAP, ALU.is_gt)
 
         def weigh(t):
             hit_adj = work.tile([P, DEPTH, W], BF16, name="hit_adj")
-            nc.vector.scalar_tensor_tensor(hit_adj[:], sizes[t][:], RELATION_GAP, adj_pieces[t][:], ALU.is_gt, ALU.mult)
+            nc.vector.tensor_tensor(hit_adj[:], hits[t][:], adj_bfs[t][:], ALU.mult)
             g, i = divmod(t, PIECES)
             for m in range(GROUP):
                 n = g * GROUP + m
@@ -103,11 +115,12 @@ def tile_labelsmoothloss_kernel(tc, base, p, adj, prob, offs, out):
             nc.vector.tensor_tensor(windows[n][:].indirect(offsets[:]), nums[n][:], inv_rel[:, n, :], ALU.mult)
             nc.sync.dma_start(out[n * P : (n + 1) * P, :], windows[n][:])
 
-
         conf_p = held.tile([P, NB, N], BF16, name="conf_p")
         nc.vector.scalar_tensor_tensor(conf_p[:], p_sb[:], PREDICT_LINE, p_sb[:], ALU.is_gt, ALU.mult)
-        rest = held.tile([P, NB, N], F32, name="rest")
-        nc.scalar.activation(rest[:], p_sb[:], COPY, bias=1.0, scale=-1.0)
+        conf = held.tile([P, NB, N], BF16, name="conf")
+        nc.vector.tensor_single_scalar(conf[:], p_sb[:], PREDICT_LINE, ALU.is_gt)
+        conf_rest = held.tile([P, NB, N], BF16, name="conf_rest")
+        nc.vector.tensor_tensor(conf_rest[:], conf[:], conf_p[:], ALU.subtract)
 
         conf_t = held.tile([P, NB, P], F32, name="conf_t")
         half_counts = held.tile([P, NB // BANK], F32, name="half_counts")
@@ -124,36 +137,45 @@ def tile_labelsmoothloss_kernel(tc, base, p, adj, prob, offs, out):
                 accum_out=half_counts[:, h : h + 1],
             )
 
-        classify(0)
-
-        conf_rest = held.tile([P, NB, N], BF16, name="conf_rest")
-        nc.vector.scalar_tensor_tensor(conf_rest[:], p_sb[:], PREDICT_LINE, rest[:], ALU.is_gt, ALU.mult)
-
-        classify(1)
-
-        den = held.tile([P, 2], F32, name="den")
-        nc.vector.tensor_scalar(den[:, 0:1], half_counts[:, 0:1], half_counts[:, 1:2], 1.0, ALU.add, ALU.add)
-        nc.vector.tensor_scalar(den[:, 1:2], half_counts[:, 0:1], half_counts[:, 1:2], 1.0, ALU.add, ALU.max)
-        inv = held.tile([P, 2], F32, name="inv")
-        nc.vector.reciprocal(inv[:], den[:])
-        slope = held.tile([P, 1], F32, name="slope")
-        nc.vector.tensor_tensor(slope[:], inv[:, 0:1], inv[:, 1:2], ALU.mult)
         inv_rel_t = held.tile([P, NB, P], F32, name="inv_rel_t")
-        nc.vector.tensor_scalar(inv_rel_t[:], conf_t[:], slope[:, 0:1], inv[:, 0:1], ALU.mult, ALU.add)
         inv_rel = held.tile([P, NB, N], F32, name="inv_rel")
-        for h in range(NB // BANK):
-            back = flips.tile([P, BANK, N], F32, name="back", tag="flip")
-            for i in range(BANK):
-                nc.tensor.transpose(back[:, i, :], inv_rel_t[:, h * BANK + i, :], identity[:])
-            nc.scalar.copy(inv_rel[:, h * BANK : (h + 1) * BANK, :], back[:])
 
-        for step in range(2, NB + PLACE_FROM):
+        def invert_counts():
+            den = held.tile([P, 2], F32, name="den")
+            nc.vector.tensor_scalar(den[:, 0:1], half_counts[:, 0:1], half_counts[:, 1:2], 1.0, ALU.add, ALU.add)
+            nc.vector.tensor_scalar(den[:, 1:2], half_counts[:, 0:1], half_counts[:, 1:2], 1.0, ALU.add, ALU.max)
+            inv = held.tile([P, 2], F32, name="inv")
+            nc.vector.reciprocal(inv[:], den[:])
+            slope = held.tile([P, 1], F32, name="slope")
+            nc.vector.tensor_tensor(slope[:], inv[:, 0:1], inv[:, 1:2], ALU.mult)
+            nc.vector.tensor_scalar(inv_rel_t[:], conf_t[:], slope[:, 0:1], inv[:, 0:1], ALU.mult, ALU.add)
+
+        def flip_back():
+            for h in range(NB // BANK):
+                back = flips.tile([P, BANK, N], F32, name="back", tag="flip")
+                for i in range(BANK):
+                    nc.tensor.transpose(back[:, i, :], inv_rel_t[:, h * BANK + i, :], identity[:])
+                nc.scalar.copy(inv_rel[:, h * BANK : (h + 1) * BANK, :], back[:])
+
+        for step in range(NB + PLACE_FROM):
             if step < NB:
-                classify(step)
-            weighed = step - WEIGH_AFTER - 1
-            if weighed >= 0 and weighed < NB and weighed % PIECES == PIECES - 1:
+                round_off(step)
+            if 0 <= step - 1 < NB:
+                subtract(step - 1)
+            if 0 <= step - 2 < NB:
+                find_hit(step - 2)
+            if 0 <= step - 1 < NB:
+                measure(step - 1)
+            if 0 <= step - 2 < NB:
+                weigh(step - 2)
+            if 0 <= step - 1 < NB:
+                find_dec(step - 1)
+            if step == 2:
+                invert_counts()
+            if step == 3:
+                flip_back()
+            weighed = step - 3
+            if 0 <= weighed < NB and weighed % PIECES == PIECES - 1:
                 collect(weighed // PIECES)
-            if step - WEIGH_AFTER < NB:
-                weigh(step - WEIGH_AFTER)
             if step >= PLACE_FROM:
                 place(step - PLACE_FROM)

@@ -4,7 +4,7 @@ from concourse.masks import make_identity
 F32, BF16, U16, I32 = mybir.dt.float32, mybir.dt.bfloat16, mybir.dt.uint16, mybir.dt.int32
 ALU = mybir.AluOpType
 ACT = mybir.ActivationFunctionType
-SIGMOID = ACT.Sigmoid
+COPY, SIGMOID = ACT.Copy, ACT.Sigmoid
 
 P = 128
 C, S, N = 1024, 256, 128
@@ -17,7 +17,10 @@ PIECES = NB // DEPTH
 PREDICT_LINE = 0.6
 RELATION_GAP = 0.05
 STEEP = 4096.0
-NO_SIGNS = 0x7FFF7FFF
+TOP = 2.0
+SCALE = TOP / RELATION_GAP
+TOP_EXPONENT_BITS = 0x40004000
+SUM_SCALE = TOP * SCALE
 PLACE_FROM = 6
 
 FLOPS = 2 * 2 * C * C * N
@@ -56,18 +59,20 @@ def tile_labelsmoothloss_kernel(tc, base, p, adj, prob, offs, out):
 
         identity = held.tile([P, P], F32, name="identity")
         make_identity(nc, identity[:])
+        scaled_identity = held.tile([P, P], F32, name="scaled_identity")
+        nc.vector.tensor_single_scalar(scaled_identity[:], identity[:], SUM_SCALE, ALU.mult)
         scratch = held.tile([P, 1], F32, name="scratch")
         nc.vector.memset(scratch[:], 0.0)
         nc.scalar.activation(scratch[:], scratch[:], SIGMOID)
 
-        priors_bf, adj_bfs, diffs, sizes, decs, hits, nums_ps, nums = {}, {}, {}, {}, {}, {}, {}, {}
+        priors_bf, adj_bfs, diffs, decs, hits, nums_ps, nums = {}, {}, {}, {}, {}, {}, {}
 
         def round_off(t):
             if t % PIECES == 0:
                 priors_bf[t // PIECES] = work.tile([P, W], BF16, name="prior_bf")
-                nc.vector.tensor_copy(priors_bf[t // PIECES][:], priors[t // PIECES][:])
+                nc.vector.tensor_single_scalar(priors_bf[t // PIECES][:], priors[t // PIECES][:], SCALE, ALU.mult)
             adj_bfs[t] = work.tile([P, DEPTH, W], BF16, name="adj_bf")
-            nc.scalar.copy(adj_bfs[t][:], adj_pieces[t][:])
+            nc.scalar.activation(adj_bfs[t][:], adj_pieces[t][:], COPY, scale=SCALE)
 
         def subtract(t):
             diffs[t] = work.tile([P, DEPTH, W], BF16, name="diff")
@@ -75,17 +80,15 @@ def tile_labelsmoothloss_kernel(tc, base, p, adj, prob, offs, out):
                 diffs[t][:], adj_bfs[t][:], priors_bf[t // PIECES][:].unsqueeze(1).to_broadcast([P, DEPTH, W]), ALU.subtract
             )
 
-        def measure(t):
-            sizes[t] = work.tile([P, DEPTH, W], BF16, name="size")
-            nc.vector.tensor_single_scalar(sizes[t][:].bitcast(I32), diffs[t][:].bitcast(I32), NO_SIGNS, ALU.bitwise_and)
-
         def find_dec(t):
             decs[t] = work.tile([P, DEPTH, W], BF16, name="dec")
-            nc.vector.tensor_single_scalar(decs[t][:], diffs[t][:], -RELATION_GAP, ALU.is_lt)
+            nc.vector.tensor_scalar(decs[t][:], diffs[t][:], -TOP, SUM_SCALE, ALU.is_lt, ALU.mult)
 
         def find_hit(t):
             hits[t] = work.tile([P, DEPTH, W], BF16, name="hit")
-            nc.vector.tensor_single_scalar(hits[t][:], sizes[t][:], RELATION_GAP, ALU.is_gt)
+            nc.vector.tensor_single_scalar(
+                hits[t][:].bitcast(I32), diffs[t][:].bitcast(I32), TOP_EXPONENT_BITS, ALU.bitwise_and
+            )
 
         def weigh(t):
             hit_adj = work.tile([P, DEPTH, W], BF16, name="hit_adj")
@@ -95,7 +98,7 @@ def tile_labelsmoothloss_kernel(tc, base, p, adj, prob, offs, out):
                 n = g * GROUP + m
                 if i == 0:
                     nums_ps[n] = sums.tile([P, N], F32, name="num_ps")
-                    nc.tensor.matmul(nums_ps[n][:], identity[:], p_sb[:, n, :], start=True, stop=False)
+                    nc.tensor.matmul(nums_ps[n][:], scaled_identity[:], p_sb[:, n, :], start=True, stop=False)
                 for b in range(DEPTH):
                     k = i * DEPTH + b
                     last = i == PIECES - 1 and b == DEPTH - 1
@@ -109,7 +112,7 @@ def tile_labelsmoothloss_kernel(tc, base, p, adj, prob, offs, out):
         def collect(g):
             for n in range(g * GROUP, (g + 1) * GROUP):
                 nums[n] = work.tile([P, N], F32, name="num")
-                nc.scalar.copy(nums[n][:], nums_ps[n][:])
+                nc.scalar.activation(nums[n][:], nums_ps[n][:], COPY, scale=1.0 / SUM_SCALE)
 
         def place(n):
             nc.vector.tensor_tensor(windows[n][:].indirect(offsets[:]), nums[n][:], inv_rel[:, n, :], ALU.mult)
@@ -165,11 +168,9 @@ def tile_labelsmoothloss_kernel(tc, base, p, adj, prob, offs, out):
             if 0 <= step - 2 < NB:
                 find_hit(step - 2)
             if 0 <= step - 1 < NB:
-                measure(step - 1)
+                find_dec(step - 1)
             if 0 <= step - 2 < NB:
                 weigh(step - 2)
-            if 0 <= step - 1 < NB:
-                find_dec(step - 1)
             if step == 2:
                 invert_counts()
             if step == 3:

@@ -4,7 +4,7 @@ from concourse.masks import make_identity
 F32, BF16, U16, I32 = mybir.dt.float32, mybir.dt.bfloat16, mybir.dt.uint16, mybir.dt.int32
 ALU = mybir.AluOpType
 ACT = mybir.ActivationFunctionType
-COPY, SIGMOID = ACT.Copy, ACT.Sigmoid
+COPY, IDENTITY, SIGMOID = ACT.Copy, ACT.Identity, ACT.Sigmoid
 
 P = 128
 C, S, N = 1024, 256, 128
@@ -70,7 +70,7 @@ def tile_labelsmoothloss_kernel(tc, base, p, adj, prob, offs, out):
         def round_off(t):
             if t % PIECES == 0:
                 priors_bf[t // PIECES] = work.tile([P, W], BF16, name="prior_bf")
-                nc.vector.tensor_single_scalar(priors_bf[t // PIECES][:], priors[t // PIECES][:], SCALE, ALU.mult)
+                nc.scalar.activation(priors_bf[t // PIECES][:], priors[t // PIECES][:], COPY, scale=SCALE)
             adj_bfs[t] = work.tile([P, DEPTH, W], BF16, name="adj_bf")
             nc.scalar.activation(adj_bfs[t][:], adj_pieces[t][:], COPY, scale=SCALE)
 
@@ -151,7 +151,7 @@ def tile_labelsmoothloss_kernel(tc, base, p, adj, prob, offs, out):
             nc.vector.reciprocal(inv[:], den[:])
             slope = held.tile([P, 1], F32, name="slope")
             nc.vector.tensor_tensor(slope[:], inv[:, 0:1], inv[:, 1:2], ALU.mult)
-            nc.vector.tensor_scalar(inv_rel_t[:], conf_t[:], slope[:, 0:1], inv[:, 0:1], ALU.mult, ALU.add)
+            nc.scalar.activation(inv_rel_t[:], conf_t[:], IDENTITY, bias=inv[:, 0:1], scale=slope[:, 0:1])
 
         def flip_back():
             for h in range(NB // BANK):

@@ -21,7 +21,7 @@ TOP = 2.0
 SCALE = TOP / RELATION_GAP
 TOP_EXPONENT_BITS = 0x40004000
 SUM_SCALE = TOP * SCALE
-PLACE_FROM = 6
+AHEAD = 3
 
 FLOPS = 2 * 2 * C * C * N
 
@@ -35,7 +35,7 @@ def tile_labelsmoothloss_kernel(tc, base, p, adj, prob, offs, out):
     with (
         tc.tile_pool(name="held", bufs=1) as held,
         tc.tile_pool(name="loads", bufs=NB) as loads,
-        tc.tile_pool(name="work", bufs=6) as work,
+        tc.tile_pool(name="work", bufs=4) as work,
         tc.psum_pool(name="sums", bufs=2 * GROUP) as sums,
         tc.psum_pool(name="flips", bufs=2) as flips,
     ):
@@ -69,9 +69,9 @@ def tile_labelsmoothloss_kernel(tc, base, p, adj, prob, offs, out):
 
         def round_off(t):
             if t % PIECES == 0:
-                priors_bf[t // PIECES] = work.tile([P, W], BF16, name="prior_bf")
+                priors_bf[t // PIECES] = loads.tile([P, W], BF16, name="prior_bf")
                 nc.scalar.activation(priors_bf[t // PIECES][:], priors[t // PIECES][:], COPY, scale=SCALE)
-            adj_bfs[t] = work.tile([P, DEPTH, W], BF16, name="adj_bf")
+            adj_bfs[t] = loads.tile([P, DEPTH, W], BF16, name="adj_bf")
             nc.scalar.activation(adj_bfs[t][:], adj_pieces[t][:], COPY, scale=SCALE)
 
         def subtract(t):
@@ -111,7 +111,7 @@ def tile_labelsmoothloss_kernel(tc, base, p, adj, prob, offs, out):
 
         def collect(g):
             for n in range(g * GROUP, (g + 1) * GROUP):
-                nums[n] = work.tile([P, N], F32, name="num")
+                nums[n] = loads.tile([P, N], F32, name="num")
                 nc.scalar.activation(nums[n][:], nums_ps[n][:], COPY, scale=1.0 / SUM_SCALE)
 
         def place(n):
@@ -127,56 +127,66 @@ def tile_labelsmoothloss_kernel(tc, base, p, adj, prob, offs, out):
 
         conf_t = held.tile([P, NB, P], F32, name="conf_t")
         half_counts = held.tile([P, NB // BANK], F32, name="half_counts")
+        flipped = []
         for h in range(NB // BANK):
             p_t = flips.tile([P, BANK, P], F32, name="p_t", tag="flip")
             for i in range(BANK):
                 nc.tensor.transpose(p_t[:, i, :], p_sb[:, h * BANK + i, :], identity[:])
-            nc.scalar.activation(
-                conf_t[:, h * BANK : (h + 1) * BANK, :],
-                p_t[:],
-                SIGMOID,
-                bias=-STEEP * PREDICT_LINE,
-                scale=STEEP,
-                accum_out=half_counts[:, h : h + 1],
-            )
+            flipped.append(p_t)
+
+        def count_confident():
+            for h in range(NB // BANK):
+                nc.scalar.activation(
+                    conf_t[:, h * BANK : (h + 1) * BANK, :],
+                    flipped[h][:],
+                    SIGMOID,
+                    bias=-STEEP * PREDICT_LINE,
+                    scale=STEEP,
+                    accum_out=half_counts[:, h : h + 1],
+                )
 
         inv_rel_t = held.tile([P, NB, P], F32, name="inv_rel_t")
         inv_rel = held.tile([P, NB, N], F32, name="inv_rel")
+        den = held.tile([P, 2], F32, name="den")
+        inv = held.tile([P, 2], F32, name="inv")
+        slope = held.tile([P, 1], F32, name="slope")
 
         def invert_counts():
-            den = held.tile([P, 2], F32, name="den")
             nc.vector.tensor_scalar(den[:, 0:1], half_counts[:, 0:1], half_counts[:, 1:2], 1.0, ALU.add, ALU.add)
             nc.vector.tensor_scalar(den[:, 1:2], half_counts[:, 0:1], half_counts[:, 1:2], 1.0, ALU.add, ALU.max)
-            inv = held.tile([P, 2], F32, name="inv")
             nc.vector.reciprocal(inv[:], den[:])
-            slope = held.tile([P, 1], F32, name="slope")
             nc.vector.tensor_tensor(slope[:], inv[:, 0:1], inv[:, 1:2], ALU.mult)
-            nc.scalar.activation(inv_rel_t[:], conf_t[:], IDENTITY, bias=inv[:, 0:1], scale=slope[:, 0:1])
 
         def flip_back():
+            nc.scalar.activation(inv_rel_t[:], conf_t[:], IDENTITY, bias=inv[:, 0:1], scale=slope[:, 0:1])
             for h in range(NB // BANK):
                 back = flips.tile([P, BANK, N], F32, name="back", tag="flip")
                 for i in range(BANK):
                     nc.tensor.transpose(back[:, i, :], inv_rel_t[:, h * BANK + i, :], identity[:])
                 nc.scalar.copy(inv_rel[:, h * BANK : (h + 1) * BANK, :], back[:])
 
-        for step in range(NB + PLACE_FROM):
+        for t in range(AHEAD):
+            round_off(t)
+        for step in range(NB + 2):
+            if step + AHEAD < NB:
+                round_off(step + AHEAD)
+            if step == 1:
+                count_confident()
             if step < NB:
-                round_off(step)
+                subtract(step)
             if 0 <= step - 1 < NB:
-                subtract(step - 1)
-            if 0 <= step - 2 < NB:
-                find_hit(step - 2)
-            if 0 <= step - 1 < NB:
+                find_hit(step - 1)
                 find_dec(step - 1)
+            if step == NB - AHEAD + 1:
+                flip_back()
             if 0 <= step - 2 < NB:
                 weigh(step - 2)
-            if step == 2:
-                invert_counts()
             if step == 3:
-                flip_back()
-            weighed = step - 3
+                invert_counts()
+            weighed = step - 4
             if 0 <= weighed < NB and weighed % PIECES == PIECES - 1:
                 collect(weighed // PIECES)
-            if step >= PLACE_FROM:
-                place(step - PLACE_FROM)
+        for n in range(NB):
+            if n == NB - GROUP:
+                collect(NB // GROUP - 1)
+            place(n)

@@ -34,7 +34,7 @@ def tile_labelsmoothloss_kernel(tc, base, p, adj, prob, offs, out):
 
     with (
         tc.tile_pool(name="held", bufs=1) as held,
-        tc.tile_pool(name="loads", bufs=NB) as loads,
+        tc.tile_pool(name="loads", bufs=NB + 2) as loads,
         tc.tile_pool(name="work", bufs=4) as work,
         tc.psum_pool(name="sums", bufs=2 * GROUP) as sums,
         tc.psum_pool(name="flips", bufs=2) as flips,
@@ -43,15 +43,21 @@ def tile_labelsmoothloss_kernel(tc, base, p, adj, prob, offs, out):
         nc.sync.dma_start(offsets[:], offs)
         p_sb = held.tile([P, NB, N], F32, name="p_sb")
         nc.sync.dma_start(p_sb[:], p_blocks)
+        pieces = [(g, i * DEPTH, DEPTH) for g in range(C // W) for i in range(PIECES)]
+        pieces = (
+            [(0, 0, DEPTH // 2), (0, DEPTH // 2, DEPTH // 2)]
+            + pieces[1:-1]
+            + [(C // W - 1, NB - DEPTH, DEPTH // 2), (C // W - 1, NB - DEPTH // 2, DEPTH // 2)]
+        )
         priors, adj_pieces, windows = [], [], []
-        for g in range(C // W):
-            prior = loads.tile([P, W], F32, name="prior")
-            nc.sync.dma_start(prior[:], prior_row[g * W : (g + 1) * W].partition_broadcast(P))
-            priors.append(prior)
-            for i in range(PIECES):
-                adj_c = loads.tile([P, DEPTH, W], F32, name="adj_c")
-                nc.sync.dma_start(adj_c[:], adj_blocks[:, i * DEPTH : (i + 1) * DEPTH, g * W : (g + 1) * W])
-                adj_pieces.append(adj_c)
+        for g, first, blocks in pieces:
+            if first == 0:
+                prior = loads.tile([P, W], F32, name="prior")
+                nc.sync.dma_start(prior[:], prior_row[g * W : (g + 1) * W].partition_broadcast(P))
+                priors.append(prior)
+            adj_c = loads.tile([P, blocks, W], F32, name="adj_c")
+            nc.sync.dma_start(adj_c[:], adj_blocks[:, first : first + blocks, g * W : (g + 1) * W])
+            adj_pieces.append(adj_c)
         for n in range(NB):
             window = loads.tile([P, S], F32, name="window")
             nc.sync.dma_start(window[:], base[n * P : (n + 1) * P, :])
@@ -68,45 +74,46 @@ def tile_labelsmoothloss_kernel(tc, base, p, adj, prob, offs, out):
         priors_bf, adj_bfs, diffs, decs, hits, nums_ps, nums = {}, {}, {}, {}, {}, {}, {}
 
         def round_off(t):
-            if t % PIECES == 0:
-                priors_bf[t // PIECES] = loads.tile([P, W], BF16, name="prior_bf")
-                nc.scalar.activation(priors_bf[t // PIECES][:], priors[t // PIECES][:], COPY, scale=SCALE)
-            adj_bfs[t] = loads.tile([P, DEPTH, W], BF16, name="adj_bf")
+            g, first, blocks = pieces[t]
+            if first == 0:
+                priors_bf[g] = loads.tile([P, W], BF16, name="prior_bf")
+                nc.scalar.activation(priors_bf[g][:], priors[g][:], COPY, scale=SCALE)
+            adj_bfs[t] = loads.tile([P, blocks, W], BF16, name="adj_bf")
             nc.scalar.activation(adj_bfs[t][:], adj_pieces[t][:], COPY, scale=SCALE)
 
         def subtract(t):
-            diffs[t] = work.tile([P, DEPTH, W], BF16, name="diff")
+            g, first, blocks = pieces[t]
+            diffs[t] = work.tile([P, blocks, W], BF16, name="diff")
             nc.vector.tensor_tensor(
-                diffs[t][:], adj_bfs[t][:], priors_bf[t // PIECES][:].unsqueeze(1).to_broadcast([P, DEPTH, W]), ALU.subtract
+                diffs[t][:], adj_bfs[t][:], priors_bf[g][:].unsqueeze(1).to_broadcast([P, blocks, W]), ALU.subtract
             )
 
         def find_dec(t):
-            decs[t] = work.tile([P, DEPTH, W], BF16, name="dec")
+            decs[t] = work.tile([P, pieces[t][2], W], BF16, name="dec")
             nc.vector.tensor_scalar(decs[t][:], diffs[t][:], -TOP, SUM_SCALE, ALU.is_lt, ALU.mult)
 
         def find_hit(t):
-            hits[t] = work.tile([P, DEPTH, W], BF16, name="hit")
+            hits[t] = work.tile([P, pieces[t][2], W], BF16, name="hit")
             nc.vector.tensor_single_scalar(
                 hits[t][:].bitcast(I32), diffs[t][:].bitcast(I32), TOP_EXPONENT_BITS, ALU.bitwise_and
             )
 
         def weigh(t):
-            hit_adj = work.tile([P, DEPTH, W], BF16, name="hit_adj")
+            g, first, blocks = pieces[t]
+            hit_adj = work.tile([P, blocks, W], BF16, name="hit_adj")
             nc.vector.tensor_tensor(hit_adj[:], hits[t][:], adj_bfs[t][:], ALU.mult)
-            g, i = divmod(t, PIECES)
             for m in range(GROUP):
                 n = g * GROUP + m
-                if i == 0:
+                if first == 0:
                     nums_ps[n] = sums.tile([P, N], F32, name="num_ps")
                     nc.tensor.matmul(nums_ps[n][:], scaled_identity[:], p_sb[:, n, :], start=True, stop=False)
-                for b in range(DEPTH):
-                    k = i * DEPTH + b
-                    last = i == PIECES - 1 and b == DEPTH - 1
+                for b in range(blocks):
+                    k = first + b
                     nc.tensor.matmul(
                         nums_ps[n][:], hit_adj[:, b, m * P : (m + 1) * P], conf_p[:, k, :], start=False, stop=False
                     )
                     nc.tensor.matmul(
-                        nums_ps[n][:], decs[t][:, b, m * P : (m + 1) * P], conf_rest[:, k, :], start=False, stop=last
+                        nums_ps[n][:], decs[t][:, b, m * P : (m + 1) * P], conf_rest[:, k, :], start=False, stop=k == NB - 1
                     )
 
         def collect(g):
@@ -165,27 +172,28 @@ def tile_labelsmoothloss_kernel(tc, base, p, adj, prob, offs, out):
                     nc.tensor.transpose(back[:, i, :], inv_rel_t[:, h * BANK + i, :], identity[:])
                 nc.scalar.copy(inv_rel[:, h * BANK : (h + 1) * BANK, :], back[:])
 
+        count = len(pieces)
         for t in range(AHEAD):
             round_off(t)
-        for step in range(NB + 2):
-            if step + AHEAD < NB:
+        for step in range(count + 2):
+            if step + AHEAD < count:
                 round_off(step + AHEAD)
-            if step == 1:
+            if step == 2:
                 count_confident()
-            if step < NB:
+            if step < count:
                 subtract(step)
-            if 0 <= step - 1 < NB:
+            if 0 <= step - 1 < count:
                 find_hit(step - 1)
                 find_dec(step - 1)
-            if step == NB - AHEAD + 1:
+            if step == count - AHEAD + 1:
                 flip_back()
-            if 0 <= step - 2 < NB:
+            if 0 <= step - 2 < count:
                 weigh(step - 2)
-            if step == 3:
+            if step == 4:
                 invert_counts()
             weighed = step - 4
-            if 0 <= weighed < NB and weighed % PIECES == PIECES - 1:
-                collect(weighed // PIECES)
+            if 0 <= weighed < count - 1 and pieces[weighed][1] + pieces[weighed][2] == NB:
+                collect(pieces[weighed][0])
         for n in range(NB):
             if n == NB - GROUP:
                 collect(NB // GROUP - 1)

@@ -30,7 +30,7 @@ def tile_labelsmoothloss_kernel(tc, base, p, adj, prob, offs, out):
     nc = tc.nc
     p_blocks = p.rearrange("(b q) j -> q b j", q=P)
     adj_blocks = adj.rearrange("(b q) c -> q b c", q=P)
-    prior_row = prob.rearrange("c o -> (c o)")
+    prior_row = prob.rearrange("c o -> o c")
 
     with (
         tc.tile_pool(name="held", bufs=1) as held,
@@ -38,23 +38,25 @@ def tile_labelsmoothloss_kernel(tc, base, p, adj, prob, offs, out):
         tc.tile_pool(name="work", bufs=4) as work,
         tc.psum_pool(name="sums", bufs=2 * GROUP) as sums,
         tc.psum_pool(name="flips", bufs=2) as flips,
+        tc.psum_pool(name="spreads", bufs=2) as spreads,
     ):
         offsets = held.tile([P, N // 16], U16, name="offsets")
         nc.sync.dma_start(offsets[:], offs)
         p_sb = held.tile([P, NB, N], F32, name="p_sb")
         nc.sync.dma_start(p_sb[:], p_blocks)
+        prior_rows = held.tile([P, C], F32, name="prior_rows")
+        nc.gpsimd.memset(prior_rows[:], 0.0)
+        nc.sync.dma_start(prior_rows[0:1, :], prior_row)
+        all_ones = held.tile([P, P], F32, name="all_ones")
+        nc.vector.memset(all_ones[:], 1.0)
         pieces = [(g, i * DEPTH, DEPTH) for g in range(C // W) for i in range(PIECES)]
         pieces = (
             [(0, 0, DEPTH // 2), (0, DEPTH // 2, DEPTH // 2)]
             + pieces[1:-1]
             + [(C // W - 1, NB - DEPTH, DEPTH // 2), (C // W - 1, NB - DEPTH // 2, DEPTH // 2)]
         )
-        priors, adj_pieces, windows = [], [], []
+        adj_pieces, windows = [], []
         for g, first, blocks in pieces:
-            if first == 0:
-                prior = loads.tile([P, W], F32, name="prior")
-                nc.sync.dma_start(prior[:], prior_row[g * W : (g + 1) * W].partition_broadcast(P))
-                priors.append(prior)
             adj_c = loads.tile([P, blocks, W], F32, name="adj_c")
             nc.sync.dma_start(adj_c[:], adj_blocks[:, first : first + blocks, g * W : (g + 1) * W])
             adj_pieces.append(adj_c)
@@ -72,12 +74,20 @@ def tile_labelsmoothloss_kernel(tc, base, p, adj, prob, offs, out):
         nc.scalar.activation(scratch[:], scratch[:], SIGMOID)
 
         priors_bf, adj_bfs, diffs, decs, hits, nums_ps, nums = {}, {}, {}, {}, {}, {}, {}
+        spread = []
+
+        def repeat_priors(g):
+            repeated = spreads.tile([P, W], F32, name="repeated")
+            nc.tensor.matmul(repeated[:], all_ones[:], prior_rows[:, g * W : (g + 1) * W], start=True, stop=True)
+            spread.append(repeated)
+
 
         def round_off(t):
             g, first, blocks = pieces[t]
             if first == 0:
+                repeat_priors(g)
                 priors_bf[g] = loads.tile([P, W], BF16, name="prior_bf")
-                nc.scalar.activation(priors_bf[g][:], priors[g][:], COPY, scale=SCALE)
+                nc.scalar.activation(priors_bf[g][:], spread[g][:], COPY, scale=SCALE)
             adj_bfs[t] = loads.tile([P, blocks, W], BF16, name="adj_bf")
             nc.scalar.activation(adj_bfs[t][:], adj_pieces[t][:], COPY, scale=SCALE)
 

@@ -4,19 +4,19 @@ from concourse.masks import make_identity
 F32, BF16, U16, I32 = mybir.dt.float32, mybir.dt.bfloat16, mybir.dt.uint16, mybir.dt.int32
 ALU = mybir.AluOpType
 ACT = mybir.ActivationFunctionType
-COPY, IDENTITY, SIGMOID = ACT.Copy, ACT.Identity, ACT.Sigmoid
+COPY, IDENTITY = ACT.Copy, ACT.Identity
 
 P = 128
 C, S, N = 1024, 256, 128
 NB = C // P
-BANK = 512 // P
+HALF = 512
+BANK = HALF // P
 W = 256
 GROUP = W // P
 DEPTH = C // W
 PIECES = NB // DEPTH
 PREDICT_LINE = 0.6
 RELATION_GAP = 0.05
-STEEP = 4096.0
 TOP = 2.0
 SCALE = TOP / RELATION_GAP
 TOP_EXPONENT_BITS = 0x40004000
@@ -40,15 +40,14 @@ def tile_labelsmoothloss_kernel(tc, base, p, adj, prob, offs, out):
         tc.psum_pool(name="flips", bufs=2) as flips,
         tc.psum_pool(name="spreads", bufs=2) as spreads,
     ):
-        offsets = held.tile([P, N // 16], U16, name="offsets")
-        nc.sync.dma_start(offsets[:], offs)
         p_sb = held.tile([P, NB, N], F32, name="p_sb")
         nc.sync.dma_start(p_sb[:], p_blocks)
         prior_rows = held.tile([P, C], F32, name="prior_rows")
         nc.gpsimd.memset(prior_rows[:], 0.0)
         nc.sync.dma_start(prior_rows[0:1, :], prior_row)
-        all_ones = held.tile([P, P], F32, name="all_ones")
+        all_ones = held.tile([P, P], BF16, name="all_ones")
         nc.vector.memset(all_ones[:], 1.0)
+        prior_rows_bf = held.tile([P, C], BF16, name="prior_rows_bf")
         pieces = [(g, i * DEPTH, DEPTH) for g in range(C // W) for i in range(PIECES)]
         pieces = (
             [(0, 0, DEPTH // 2), (0, DEPTH // 2, DEPTH // 2)]
@@ -60,6 +59,8 @@ def tile_labelsmoothloss_kernel(tc, base, p, adj, prob, offs, out):
             adj_c = loads.tile([P, blocks, W], F32, name="adj_c")
             nc.sync.dma_start(adj_c[:], adj_blocks[:, first : first + blocks, g * W : (g + 1) * W])
             adj_pieces.append(adj_c)
+        offsets = held.tile([P, N // 16], U16, name="offsets")
+        nc.sync.dma_start(offsets[:], offs)
         for n in range(NB):
             window = loads.tile([P, S], F32, name="window")
             nc.sync.dma_start(window[:], base[n * P : (n + 1) * P, :])
@@ -69,25 +70,28 @@ def tile_labelsmoothloss_kernel(tc, base, p, adj, prob, offs, out):
         make_identity(nc, identity[:])
         scaled_identity = held.tile([P, P], F32, name="scaled_identity")
         nc.vector.tensor_single_scalar(scaled_identity[:], identity[:], SUM_SCALE, ALU.mult)
+        identity_bf = held.tile([P, P], BF16, name="identity_bf")
+        make_identity(nc, identity_bf[:])
         scratch = held.tile([P, 1], F32, name="scratch")
         nc.vector.memset(scratch[:], 0.0)
-        nc.scalar.activation(scratch[:], scratch[:], SIGMOID)
+        nc.scalar.activation(scratch[:], scratch[:], COPY)
 
         priors_bf, adj_bfs, diffs, decs, hits, nums_ps, nums = {}, {}, {}, {}, {}, {}, {}
-        spread = []
 
-        def repeat_priors(g):
-            repeated = spreads.tile([P, W], F32, name="repeated")
-            nc.tensor.matmul(repeated[:], all_ones[:], prior_rows[:, g * W : (g + 1) * W], start=True, stop=True)
-            spread.append(repeated)
+        def repeat_priors(begin, end):
+            nc.vector.tensor_single_scalar(prior_rows_bf[:, begin:end], prior_rows[:, begin:end], SCALE, ALU.mult)
+            repeated = spreads.tile([P, end - begin], BF16, name="repeated")
+            for c in range(begin, end, HALF):
+                width = min(HALF, end - c)
+                nc.tensor.matmul(
+                    repeated[:, c - begin : c - begin + width], all_ones[:], prior_rows_bf[:, c : c + width], start=True, stop=True
+                )
+            for g in range(begin // W, end // W):
+                priors_bf[g] = repeated[:, g * W - begin : (g + 1) * W - begin]
 
 
         def round_off(t):
             g, first, blocks = pieces[t]
-            if first == 0:
-                repeat_priors(g)
-                priors_bf[g] = loads.tile([P, W], BF16, name="prior_bf")
-                nc.scalar.activation(priors_bf[g][:], spread[g][:], COPY, scale=SCALE)
             adj_bfs[t] = loads.tile([P, blocks, W], BF16, name="adj_bf")
             nc.scalar.activation(adj_bfs[t][:], adj_pieces[t][:], COPY, scale=SCALE)
 
@@ -95,7 +99,7 @@ def tile_labelsmoothloss_kernel(tc, base, p, adj, prob, offs, out):
             g, first, blocks = pieces[t]
             diffs[t] = work.tile([P, blocks, W], BF16, name="diff")
             nc.vector.tensor_tensor(
-                diffs[t][:], adj_bfs[t][:], priors_bf[g][:].unsqueeze(1).to_broadcast([P, blocks, W]), ALU.subtract
+                diffs[t][:], adj_bfs[t][:], priors_bf[g].unsqueeze(1).to_broadcast([P, blocks, W]), ALU.subtract
             )
 
         def find_dec(t):
@@ -135,75 +139,74 @@ def tile_labelsmoothloss_kernel(tc, base, p, adj, prob, offs, out):
             nc.vector.tensor_tensor(windows[n][:].indirect(offsets[:]), nums[n][:], inv_rel[:, n, :], ALU.mult)
             nc.sync.dma_start(out[n * P : (n + 1) * P, :], windows[n][:])
 
-        conf_p = held.tile([P, NB, N], BF16, name="conf_p")
-        nc.vector.scalar_tensor_tensor(conf_p[:], p_sb[:], PREDICT_LINE, p_sb[:], ALU.is_gt, ALU.mult)
         conf = held.tile([P, NB, N], BF16, name="conf")
         nc.vector.tensor_single_scalar(conf[:], p_sb[:], PREDICT_LINE, ALU.is_gt)
+        repeat_priors(0, W)
+        conf_p = held.tile([P, NB, N], BF16, name="conf_p")
+        nc.vector.tensor_tensor(conf_p[:], conf[:], p_sb[:], ALU.mult)
         conf_rest = held.tile([P, NB, N], BF16, name="conf_rest")
         nc.vector.tensor_tensor(conf_rest[:], conf[:], conf_p[:], ALU.subtract)
 
-        conf_t = held.tile([P, NB, P], F32, name="conf_t")
-        half_counts = held.tile([P, NB // BANK], F32, name="half_counts")
-        flipped = []
-        for h in range(NB // BANK):
-            p_t = flips.tile([P, BANK, P], F32, name="p_t", tag="flip")
-            for i in range(BANK):
-                nc.tensor.transpose(p_t[:, i, :], p_sb[:, h * BANK + i, :], identity[:])
-            flipped.append(p_t)
-
-        def count_confident():
-            for h in range(NB // BANK):
-                nc.scalar.activation(
-                    conf_t[:, h * BANK : (h + 1) * BANK, :],
-                    flipped[h][:],
-                    SIGMOID,
-                    bias=-STEEP * PREDICT_LINE,
-                    scale=STEEP,
-                    accum_out=half_counts[:, h : h + 1],
-                )
+        conf_t = flips.tile([P, NB, P], BF16, name="conf_t", tag="flip")
+        for n in range(NB):
+            nc.tensor.transpose(conf_t[:, n, :], conf[:, n, :], identity_bf[:])
+        count = flips.tile([P, 1], F32, name="count", tag="flip")
+        for k in range(NB):
+            nc.tensor.matmul(count[:], conf[:, k, :], all_ones[:, 0:1], start=k == 0, stop=k == NB - 1)
 
         inv_rel_t = held.tile([P, NB, P], F32, name="inv_rel_t")
         inv_rel = held.tile([P, NB, N], F32, name="inv_rel")
         den = held.tile([P, 2], F32, name="den")
         inv = held.tile([P, 2], F32, name="inv")
         slope = held.tile([P, 1], F32, name="slope")
+        backs = []
 
         def invert_counts():
-            nc.vector.tensor_scalar(den[:, 0:1], half_counts[:, 0:1], half_counts[:, 1:2], 1.0, ALU.add, ALU.add)
-            nc.vector.tensor_scalar(den[:, 1:2], half_counts[:, 0:1], half_counts[:, 1:2], 1.0, ALU.add, ALU.max)
+            nc.vector.tensor_single_scalar(den[:, 0:1], count[:], 1.0, ALU.add)
+            nc.vector.tensor_single_scalar(den[:, 1:2], count[:], 1.0, ALU.max)
             nc.vector.reciprocal(inv[:], den[:])
             nc.vector.tensor_tensor(slope[:], inv[:, 0:1], inv[:, 1:2], ALU.mult)
 
-        def flip_back():
+        def spread_inverse():
             nc.scalar.activation(inv_rel_t[:], conf_t[:], IDENTITY, bias=inv[:, 0:1], scale=slope[:, 0:1])
+
+        def flip_back():
             for h in range(NB // BANK):
                 back = flips.tile([P, BANK, N], F32, name="back", tag="flip")
                 for i in range(BANK):
                     nc.tensor.transpose(back[:, i, :], inv_rel_t[:, h * BANK + i, :], identity[:])
-                nc.scalar.copy(inv_rel[:, h * BANK : (h + 1) * BANK, :], back[:])
+                backs.append(back)
 
-        count = len(pieces)
+        def copy_back():
+            for h in range(NB // BANK):
+                nc.scalar.copy(inv_rel[:, h * BANK : (h + 1) * BANK, :], backs[h][:])
+
+        n_pieces = len(pieces)
         for t in range(AHEAD):
             round_off(t)
-        for step in range(count + 2):
-            if step + AHEAD < count:
+        for step in range(n_pieces + 2):
+            if step + AHEAD < n_pieces:
                 round_off(step + AHEAD)
-            if step == 2:
-                count_confident()
-            if step < count:
+            if step == n_pieces // 2 - 1:
+                spread_inverse()
+            if step < n_pieces:
                 subtract(step)
-            if 0 <= step - 1 < count:
+            if step == 0:
+                repeat_priors(W, C)
+            if step == 1:
+                invert_counts()
+            if 0 <= step - 1 < n_pieces:
                 find_hit(step - 1)
                 find_dec(step - 1)
-            if step == count - AHEAD + 1:
-                flip_back()
-            if 0 <= step - 2 < count:
+            if 0 <= step - 2 < n_pieces:
                 weigh(step - 2)
-            if step == 4:
-                invert_counts()
+            if step == n_pieces // 2 + 1:
+                flip_back()
             weighed = step - 4
-            if 0 <= weighed < count - 1 and pieces[weighed][1] + pieces[weighed][2] == NB:
+            if 0 <= weighed < n_pieces - 1 and pieces[weighed][1] + pieces[weighed][2] == NB:
                 collect(pieces[weighed][0])
+            if step == n_pieces - AHEAD:
+                copy_back()
         for n in range(NB):
             if n == NB - GROUP:
                 collect(NB // GROUP - 1)

@@ -11,6 +11,7 @@ C, S, N = 1024, 256, 128
 NB = C // P
 HALF = 512
 BANK = HALF // P
+HALF_BLOCKS = NB // 2
 W = 256
 GROUP = W // P
 DEPTH = C // W
@@ -30,24 +31,25 @@ def tile_labelsmoothloss_kernel(tc, base, p, adj, prob, offs, out):
     nc = tc.nc
     p_blocks = p.rearrange("(b q) j -> q b j", q=P)
     adj_blocks = adj.rearrange("(b q) c -> q b c", q=P)
-    prior_row = prob.rearrange("c o -> o c")
+    prior_blocks = prob.rearrange("(b q) o -> b (q o)", q=P)
 
     with (
         tc.tile_pool(name="held", bufs=1) as held,
         tc.tile_pool(name="loads", bufs=NB + 2) as loads,
-        tc.tile_pool(name="work", bufs=4) as work,
+        tc.tile_pool(name="work", bufs=8) as work,
         tc.psum_pool(name="sums", bufs=2 * GROUP) as sums,
         tc.psum_pool(name="flips", bufs=2) as flips,
         tc.psum_pool(name="spreads", bufs=2) as spreads,
     ):
         p_sb = held.tile([P, NB, N], F32, name="p_sb")
-        nc.sync.dma_start(p_sb[:], p_blocks)
-        prior_rows = held.tile([P, C], F32, name="prior_rows")
+        for h in range(0, NB, HALF_BLOCKS):
+            nc.sync.dma_start(p_sb[:, h : h + HALF_BLOCKS, :], p_blocks[:, h : h + HALF_BLOCKS, :])
+        prior_rows = held.tile([P, P], F32, name="prior_rows")
         nc.gpsimd.memset(prior_rows[:], 0.0)
-        nc.sync.dma_start(prior_rows[0:1, :], prior_row)
+        nc.sync.dma_start(prior_rows[0:NB, :], prior_blocks)
         all_ones = held.tile([P, P], BF16, name="all_ones")
         nc.vector.memset(all_ones[:], 1.0)
-        prior_rows_bf = held.tile([P, C], BF16, name="prior_rows_bf")
+        prior_rows_bf = held.tile([P, P], BF16, name="prior_rows_bf")
         pieces = [(g, i * DEPTH, DEPTH) for g in range(C // W) for i in range(PIECES)]
         pieces = (
             [(0, 0, DEPTH // 2), (0, DEPTH // 2, DEPTH // 2)]
@@ -66,12 +68,12 @@ def tile_labelsmoothloss_kernel(tc, base, p, adj, prob, offs, out):
             nc.sync.dma_start(window[:], base[n * P : (n + 1) * P, :])
             windows.append(window)
 
+        identity_bf = held.tile([P, P], BF16, name="identity_bf")
+        make_identity(nc, identity_bf[:])
         identity = held.tile([P, P], F32, name="identity")
         make_identity(nc, identity[:])
         scaled_identity = held.tile([P, P], F32, name="scaled_identity")
         nc.vector.tensor_single_scalar(scaled_identity[:], identity[:], SUM_SCALE, ALU.mult)
-        identity_bf = held.tile([P, P], BF16, name="identity_bf")
-        make_identity(nc, identity_bf[:])
         scratch = held.tile([P, 1], F32, name="scratch")
         nc.vector.memset(scratch[:], 0.0)
         nc.scalar.activation(scratch[:], scratch[:], COPY)
@@ -79,12 +81,10 @@ def tile_labelsmoothloss_kernel(tc, base, p, adj, prob, offs, out):
         priors_bf, adj_bfs, diffs, decs, hits, nums_ps, nums = {}, {}, {}, {}, {}, {}, {}
 
         def repeat_priors(begin, end):
-            nc.vector.tensor_single_scalar(prior_rows_bf[:, begin:end], prior_rows[:, begin:end], SCALE, ALU.mult)
             repeated = spreads.tile([P, end - begin], BF16, name="repeated")
-            for c in range(begin, end, HALF):
-                width = min(HALF, end - c)
+            for c in range(begin, end, P):
                 nc.tensor.matmul(
-                    repeated[:, c - begin : c - begin + width], all_ones[:], prior_rows_bf[:, c : c + width], start=True, stop=True
+                    repeated[:, c - begin : c - begin + P], identity_bf[:, c // P : c // P + 1].to_broadcast([P, P]), prior_rows_bf[:], start=True, stop=True
                 )
             for g in range(begin // W, end // W):
                 priors_bf[g] = repeated[:, g * W - begin : (g + 1) * W - begin]
@@ -139,13 +139,19 @@ def tile_labelsmoothloss_kernel(tc, base, p, adj, prob, offs, out):
             nc.vector.tensor_tensor(windows[n][:].indirect(offsets[:]), nums[n][:], inv_rel[:, n, :], ALU.mult)
             nc.sync.dma_start(out[n * P : (n + 1) * P, :], windows[n][:])
 
-        conf = held.tile([P, NB, N], BF16, name="conf")
-        nc.vector.tensor_single_scalar(conf[:], p_sb[:], PREDICT_LINE, ALU.is_gt)
+        nc.vector.tensor_single_scalar(prior_rows_bf[:], prior_rows[:], SCALE, ALU.mult)
         repeat_priors(0, W)
+        repeat_priors(W, C)
+        p_bf = held.tile([P, NB, N], BF16, name="p_bf")
+        conf = held.tile([P, NB, N], BF16, name="conf")
         conf_p = held.tile([P, NB, N], BF16, name="conf_p")
-        nc.vector.tensor_tensor(conf_p[:], conf[:], p_sb[:], ALU.mult)
         conf_rest = held.tile([P, NB, N], BF16, name="conf_rest")
-        nc.vector.tensor_tensor(conf_rest[:], conf[:], conf_p[:], ALU.subtract)
+        for h in range(0, NB, HALF_BLOCKS):
+            half = slice(h, h + HALF_BLOCKS)
+            nc.scalar.activation(p_bf[:, half, :], p_sb[:, half, :], COPY)
+            nc.vector.tensor_single_scalar(conf[:, half, :], p_bf[:, half, :], PREDICT_LINE, ALU.is_gt)
+            nc.vector.tensor_tensor(conf_p[:, half, :], conf[:, half, :], p_bf[:, half, :], ALU.mult)
+            nc.vector.tensor_tensor(conf_rest[:, half, :], conf[:, half, :], conf_p[:, half, :], ALU.subtract)
 
         conf_t = flips.tile([P, NB, P], BF16, name="conf_t", tag="flip")
         for n in range(NB):
@@ -191,8 +197,6 @@ def tile_labelsmoothloss_kernel(tc, base, p, adj, prob, offs, out):
                 spread_inverse()
             if step < n_pieces:
                 subtract(step)
-            if step == 0:
-                repeat_priors(W, C)
             if step == 1:
                 invert_counts()
             if 0 <= step - 1 < n_pieces:

@@ -12,7 +12,7 @@ NB = C // P
 HALF = 512
 BANK = HALF // P
 HALF_BLOCKS = NB // 2
-W = 256
+W = 512
 GROUP = W // P
 DEPTH = C // W
 PIECES = NB // DEPTH
@@ -31,25 +31,22 @@ def tile_labelsmoothloss_kernel(tc, base, p, adj, prob, offs, out):
     nc = tc.nc
     p_blocks = p.rearrange("(b q) j -> q b j", q=P)
     adj_blocks = adj.rearrange("(b q) c -> q b c", q=P)
-    prior_blocks = prob.rearrange("(b q) o -> b (q o)", q=P)
+    prior_row = prob.rearrange("c o -> o c")
 
     with (
         tc.tile_pool(name="held", bufs=1) as held,
         tc.tile_pool(name="loads", bufs=NB + 2) as loads,
+        tc.tile_pool(name="rounded", bufs=5) as rounded,
         tc.tile_pool(name="work", bufs=8) as work,
-        tc.psum_pool(name="sums", bufs=2 * GROUP) as sums,
-        tc.psum_pool(name="flips", bufs=2) as flips,
-        tc.psum_pool(name="spreads", bufs=2) as spreads,
+        tc.psum_pool(name="banks", bufs=8) as banks,
     ):
-        p_sb = held.tile([P, NB, N], F32, name="p_sb")
-        for h in range(0, NB, HALF_BLOCKS):
-            nc.sync.dma_start(p_sb[:, h : h + HALF_BLOCKS, :], p_blocks[:, h : h + HALF_BLOCKS, :])
-        prior_rows = held.tile([P, P], F32, name="prior_rows")
-        nc.gpsimd.memset(prior_rows[:], 0.0)
-        nc.sync.dma_start(prior_rows[0:NB, :], prior_blocks)
+        priors = held.tile([1, C], F32, name="priors")
+        nc.sync.dma_start(priors[:], prior_row)
+        prior_rows_bf = held.tile([P, C], BF16, name="prior_rows_bf")
+        nc.vector.memset(prior_rows_bf[:], 0.0)
         all_ones = held.tile([P, P], BF16, name="all_ones")
         nc.vector.memset(all_ones[:], 1.0)
-        prior_rows_bf = held.tile([P, P], BF16, name="prior_rows_bf")
+        p_sb = held.tile([P, NB, N], F32, name="p_sb")
         pieces = [(g, i * DEPTH, DEPTH) for g in range(C // W) for i in range(PIECES)]
         pieces = (
             [(0, 0, DEPTH // 2), (0, DEPTH // 2, DEPTH // 2)]
@@ -61,6 +58,9 @@ def tile_labelsmoothloss_kernel(tc, base, p, adj, prob, offs, out):
             adj_c = loads.tile([P, blocks, W], F32, name="adj_c")
             nc.sync.dma_start(adj_c[:], adj_blocks[:, first : first + blocks, g * W : (g + 1) * W])
             adj_pieces.append(adj_c)
+            if len(adj_pieces) == 1:
+                for h in range(0, NB, HALF_BLOCKS):
+                    nc.sync.dma_start(p_sb[:, h : h + HALF_BLOCKS, :], p_blocks[:, h : h + HALF_BLOCKS, :])
         offsets = held.tile([P, N // 16], U16, name="offsets")
         nc.sync.dma_start(offsets[:], offs)
         for n in range(NB):
@@ -71,35 +71,31 @@ def tile_labelsmoothloss_kernel(tc, base, p, adj, prob, offs, out):
         identity_bf = held.tile([P, P], BF16, name="identity_bf")
         make_identity(nc, identity_bf[:])
         identity = held.tile([P, P], F32, name="identity")
-        make_identity(nc, identity[:])
+        nc.vector.tensor_copy(identity[:], identity_bf[:])
         scaled_identity = held.tile([P, P], F32, name="scaled_identity")
-        nc.vector.tensor_single_scalar(scaled_identity[:], identity[:], SUM_SCALE, ALU.mult)
+        nc.vector.tensor_single_scalar(scaled_identity[:], identity_bf[:], SUM_SCALE, ALU.mult)
         scratch = held.tile([P, 1], F32, name="scratch")
         nc.vector.memset(scratch[:], 0.0)
         nc.scalar.activation(scratch[:], scratch[:], COPY)
 
         priors_bf, adj_bfs, diffs, decs, hits, nums_ps, nums = {}, {}, {}, {}, {}, {}, {}
 
-        def repeat_priors(begin, end):
-            repeated = spreads.tile([P, end - begin], BF16, name="repeated")
-            for c in range(begin, end, P):
-                nc.tensor.matmul(
-                    repeated[:, c - begin : c - begin + P], identity_bf[:, c // P : c // P + 1].to_broadcast([P, P]), prior_rows_bf[:], start=True, stop=True
-                )
-            for g in range(begin // W, end // W):
-                priors_bf[g] = repeated[:, g * W - begin : (g + 1) * W - begin]
-
+        def repeat_priors(g):
+            columns = slice(g * W, (g + 1) * W)
+            nc.vector.tensor_single_scalar(prior_rows_bf[0:1, columns], priors[:, columns], SCALE, ALU.mult)
+            priors_bf[g] = banks.tile([P, W], BF16, name="repeated", tag="bank")
+            nc.tensor.matmul(priors_bf[g][:], all_ones[:], prior_rows_bf[:, columns], start=True, stop=True)
 
         def round_off(t):
             g, first, blocks = pieces[t]
-            adj_bfs[t] = loads.tile([P, blocks, W], BF16, name="adj_bf")
+            adj_bfs[t] = rounded.tile([P, blocks, W], BF16, name="adj_bf")
             nc.scalar.activation(adj_bfs[t][:], adj_pieces[t][:], COPY, scale=SCALE)
 
         def subtract(t):
             g, first, blocks = pieces[t]
             diffs[t] = work.tile([P, blocks, W], BF16, name="diff")
             nc.vector.tensor_tensor(
-                diffs[t][:], adj_bfs[t][:], priors_bf[g].unsqueeze(1).to_broadcast([P, blocks, W]), ALU.subtract
+                diffs[t][:], adj_bfs[t][:], priors_bf[g][:].unsqueeze(1).to_broadcast([P, blocks, W]), ALU.subtract
             )
 
         def find_dec(t):
@@ -119,12 +115,13 @@ def tile_labelsmoothloss_kernel(tc, base, p, adj, prob, offs, out):
             for m in range(GROUP):
                 n = g * GROUP + m
                 if first == 0:
-                    nums_ps[n] = sums.tile([P, N], F32, name="num_ps")
-                    nc.tensor.matmul(nums_ps[n][:], scaled_identity[:], p_sb[:, n, :], start=True, stop=False)
+                    nums_ps[n] = banks.tile([P, N], F32, name="num_ps", tag="bank")
+                if first == DEPTH:
+                    nc.tensor.matmul(nums_ps[n][:], scaled_identity[:], p_sb[:, n, :], start=False, stop=False)
                 for b in range(blocks):
                     k = first + b
                     nc.tensor.matmul(
-                        nums_ps[n][:], hit_adj[:, b, m * P : (m + 1) * P], conf_p[:, k, :], start=False, stop=False
+                        nums_ps[n][:], hit_adj[:, b, m * P : (m + 1) * P], conf_p[:, k, :], start=k == 0, stop=False
                     )
                     nc.tensor.matmul(
                         nums_ps[n][:], decs[t][:, b, m * P : (m + 1) * P], conf_rest[:, k, :], start=False, stop=k == NB - 1
@@ -139,9 +136,12 @@ def tile_labelsmoothloss_kernel(tc, base, p, adj, prob, offs, out):
             nc.vector.tensor_tensor(windows[n][:].indirect(offsets[:]), nums[n][:], inv_rel[:, n, :], ALU.mult)
             nc.sync.dma_start(out[n * P : (n + 1) * P, :], windows[n][:])
 
-        nc.vector.tensor_single_scalar(prior_rows_bf[:], prior_rows[:], SCALE, ALU.mult)
-        repeat_priors(0, W)
-        repeat_priors(W, C)
+        repeat_priors(0)
+        repeat_priors(1)
+        round_off(0)
+        subtract(0)
+        find_hit(0)
+        find_dec(0)
         p_bf = held.tile([P, NB, N], BF16, name="p_bf")
         conf = held.tile([P, NB, N], BF16, name="conf")
         conf_p = held.tile([P, NB, N], BF16, name="conf_p")
@@ -153,10 +153,10 @@ def tile_labelsmoothloss_kernel(tc, base, p, adj, prob, offs, out):
             nc.vector.tensor_tensor(conf_p[:, half, :], conf[:, half, :], p_bf[:, half, :], ALU.mult)
             nc.vector.tensor_tensor(conf_rest[:, half, :], conf[:, half, :], conf_p[:, half, :], ALU.subtract)
 
-        conf_t = flips.tile([P, NB, P], BF16, name="conf_t", tag="flip")
+        conf_t = banks.tile([P, NB, P], BF16, name="conf_t", tag="bank")
         for n in range(NB):
             nc.tensor.transpose(conf_t[:, n, :], conf[:, n, :], identity_bf[:])
-        count = flips.tile([P, 1], F32, name="count", tag="flip")
+        count = banks.tile([P, 1], F32, name="count", tag="bank")
         for k in range(NB):
             nc.tensor.matmul(count[:], conf[:, k, :], all_ones[:, 0:1], start=k == 0, stop=k == NB - 1)
 
@@ -167,18 +167,17 @@ def tile_labelsmoothloss_kernel(tc, base, p, adj, prob, offs, out):
         slope = held.tile([P, 1], F32, name="slope")
         backs = []
 
-        def invert_counts():
-            nc.vector.tensor_single_scalar(den[:, 0:1], count[:], 1.0, ALU.add)
-            nc.vector.tensor_single_scalar(den[:, 1:2], count[:], 1.0, ALU.max)
-            nc.vector.reciprocal(inv[:], den[:])
-            nc.vector.tensor_tensor(slope[:], inv[:, 0:1], inv[:, 1:2], ALU.mult)
+        nc.vector.tensor_single_scalar(den[:, 0:1], count[:], 1.0, ALU.add)
+        nc.vector.tensor_single_scalar(den[:, 1:2], count[:], 1.0, ALU.max)
+        nc.vector.reciprocal(inv[:], den[:])
+        nc.vector.tensor_tensor(slope[:], inv[:, 0:1], inv[:, 1:2], ALU.mult)
 
         def spread_inverse():
             nc.scalar.activation(inv_rel_t[:], conf_t[:], IDENTITY, bias=inv[:, 0:1], scale=slope[:, 0:1])
 
         def flip_back():
             for h in range(NB // BANK):
-                back = flips.tile([P, BANK, N], F32, name="back", tag="flip")
+                back = banks.tile([P, BANK, N], F32, name="back", tag="bank")
                 for i in range(BANK):
                     nc.tensor.transpose(back[:, i, :], inv_rel_t[:, h * BANK + i, :], identity[:])
                 backs.append(back)
@@ -188,28 +187,26 @@ def tile_labelsmoothloss_kernel(tc, base, p, adj, prob, offs, out):
                 nc.scalar.copy(inv_rel[:, h * BANK : (h + 1) * BANK, :], backs[h][:])
 
         n_pieces = len(pieces)
-        for t in range(AHEAD):
+        for t in range(1, AHEAD):
             round_off(t)
         for step in range(n_pieces + 2):
             if step + AHEAD < n_pieces:
                 round_off(step + AHEAD)
-            if step == n_pieces // 2 - 1:
-                spread_inverse()
-            if step < n_pieces:
-                subtract(step)
             if step == 1:
-                invert_counts()
-            if 0 <= step - 1 < n_pieces:
+                spread_inverse()
+            if 1 <= step < n_pieces:
+                subtract(step)
+            if 1 <= step - 1 < n_pieces:
                 find_hit(step - 1)
                 find_dec(step - 1)
             if 0 <= step - 2 < n_pieces:
                 weigh(step - 2)
-            if step == n_pieces // 2 + 1:
+            if step == n_pieces // 2:
                 flip_back()
             weighed = step - 4
             if 0 <= weighed < n_pieces - 1 and pieces[weighed][1] + pieces[weighed][2] == NB:
                 collect(pieces[weighed][0])
-            if step == n_pieces - AHEAD:
+            if step == n_pieces - AHEAD + 1:
                 copy_back()
         for n in range(NB):
             if n == NB - GROUP:

@@ -22,7 +22,7 @@ TOP = 2.0
 SCALE = TOP / RELATION_GAP
 TOP_EXPONENT_BITS = 0x40004000
 SUM_SCALE = TOP * SCALE
-AHEAD = 3
+AHEAD = 2
 
 FLOPS = 2 * 2 * C * C * N
 
@@ -36,9 +36,9 @@ def tile_labelsmoothloss_kernel(tc, base, p, adj, prob, offs, out):
     with (
         tc.tile_pool(name="held", bufs=1) as held,
         tc.tile_pool(name="loads", bufs=NB + 2) as loads,
-        tc.tile_pool(name="rounded", bufs=5) as rounded,
         tc.tile_pool(name="work", bufs=8) as work,
-        tc.psum_pool(name="banks", bufs=8) as banks,
+        tc.psum_pool(name="banks", bufs=7) as banks,
+        tc.psum_pool(name="backs", bufs=1) as backs,
     ):
         priors = held.tile([1, C], F32, name="priors")
         nc.sync.dma_start(priors[:], prior_row)
@@ -47,6 +47,8 @@ def tile_labelsmoothloss_kernel(tc, base, p, adj, prob, offs, out):
         all_ones = held.tile([P, P], BF16, name="all_ones")
         nc.vector.memset(all_ones[:], 1.0)
         p_sb = held.tile([P, NB, N], F32, name="p_sb")
+        early, late = slice(0, HALF_BLOCKS), slice(HALF_BLOCKS, NB)
+        nc.sync.dma_start(p_sb[:, early, :], p_blocks[:, early, :])
         pieces = [(g, i * DEPTH, DEPTH) for g in range(C // W) for i in range(PIECES)]
         pieces = (
             [(0, 0, DEPTH // 2), (0, DEPTH // 2, DEPTH // 2)]
@@ -59,8 +61,7 @@ def tile_labelsmoothloss_kernel(tc, base, p, adj, prob, offs, out):
             nc.sync.dma_start(adj_c[:], adj_blocks[:, first : first + blocks, g * W : (g + 1) * W])
             adj_pieces.append(adj_c)
             if len(adj_pieces) == 1:
-                for h in range(0, NB, HALF_BLOCKS):
-                    nc.sync.dma_start(p_sb[:, h : h + HALF_BLOCKS, :], p_blocks[:, h : h + HALF_BLOCKS, :])
+                nc.sync.dma_start(p_sb[:, late, :], p_blocks[:, late, :])
         offsets = held.tile([P, N // 16], U16, name="offsets")
         nc.sync.dma_start(offsets[:], offs)
         for n in range(NB):
@@ -71,9 +72,9 @@ def tile_labelsmoothloss_kernel(tc, base, p, adj, prob, offs, out):
         identity_bf = held.tile([P, P], BF16, name="identity_bf")
         make_identity(nc, identity_bf[:])
         identity = held.tile([P, P], F32, name="identity")
-        nc.vector.tensor_copy(identity[:], identity_bf[:])
+        nc.gpsimd.tensor_copy(identity[:], identity_bf[:])
         scaled_identity = held.tile([P, P], F32, name="scaled_identity")
-        nc.vector.tensor_single_scalar(scaled_identity[:], identity_bf[:], SUM_SCALE, ALU.mult)
+        nc.gpsimd.tensor_single_scalar(scaled_identity[:], identity_bf[:], SUM_SCALE, ALU.mult)
         scratch = held.tile([P, 1], F32, name="scratch")
         nc.vector.memset(scratch[:], 0.0)
         nc.scalar.activation(scratch[:], scratch[:], COPY)
@@ -88,8 +89,11 @@ def tile_labelsmoothloss_kernel(tc, base, p, adj, prob, offs, out):
 
         def round_off(t):
             g, first, blocks = pieces[t]
-            adj_bfs[t] = rounded.tile([P, blocks, W], BF16, name="adj_bf")
-            nc.scalar.activation(adj_bfs[t][:], adj_pieces[t][:], COPY, scale=SCALE)
+            adj_bfs[t] = loads.tile([P, blocks, W], BF16, name="adj_bf")
+            if t == 0:
+                nc.vector.tensor_single_scalar(adj_bfs[t][:], adj_pieces[t][:], SCALE, ALU.mult)
+            else:
+                nc.scalar.activation(adj_bfs[t][:], adj_pieces[t][:], COPY, scale=SCALE)
 
         def subtract(t):
             g, first, blocks = pieces[t]
@@ -112,16 +116,21 @@ def tile_labelsmoothloss_kernel(tc, base, p, adj, prob, offs, out):
             g, first, blocks = pieces[t]
             hit_adj = work.tile([P, blocks, W], BF16, name="hit_adj")
             nc.vector.tensor_tensor(hit_adj[:], hits[t][:], adj_bfs[t][:], ALU.mult)
+            p_joins = DEPTH if g == 0 else 0
             for m in range(GROUP):
                 n = g * GROUP + m
                 if first == 0:
                     nums_ps[n] = banks.tile([P, N], F32, name="num_ps", tag="bank")
-                if first == DEPTH:
-                    nc.tensor.matmul(nums_ps[n][:], scaled_identity[:], p_sb[:, n, :], start=False, stop=False)
+                if first == p_joins:
+                    nc.tensor.matmul(nums_ps[n][:], scaled_identity[:], p_sb[:, n, :], start=first == 0, stop=False)
                 for b in range(blocks):
                     k = first + b
                     nc.tensor.matmul(
-                        nums_ps[n][:], hit_adj[:, b, m * P : (m + 1) * P], conf_p[:, k, :], start=k == 0, stop=False
+                        nums_ps[n][:],
+                        hit_adj[:, b, m * P : (m + 1) * P],
+                        conf_p[:, k, :],
+                        start=k == 0 and p_joins > 0,
+                        stop=False,
                     )
                     nc.tensor.matmul(
                         nums_ps[n][:], decs[t][:, b, m * P : (m + 1) * P], conf_rest[:, k, :], start=False, stop=k == NB - 1
@@ -138,53 +147,49 @@ def tile_labelsmoothloss_kernel(tc, base, p, adj, prob, offs, out):
 
         repeat_priors(0)
         repeat_priors(1)
-        round_off(0)
-        subtract(0)
-        find_hit(0)
-        find_dec(0)
         p_bf = held.tile([P, NB, N], BF16, name="p_bf")
         conf = held.tile([P, NB, N], BF16, name="conf")
         conf_p = held.tile([P, NB, N], BF16, name="conf_p")
         conf_rest = held.tile([P, NB, N], BF16, name="conf_rest")
-        for h in range(0, NB, HALF_BLOCKS):
-            half = slice(h, h + HALF_BLOCKS)
+        for half in (early, late):
+            nc.vector.tensor_single_scalar(conf[:, half, :], p_sb[:, half, :], PREDICT_LINE, ALU.is_gt)
+            if half == early:
+                round_off(0)
             nc.scalar.activation(p_bf[:, half, :], p_sb[:, half, :], COPY)
-            nc.vector.tensor_single_scalar(conf[:, half, :], p_bf[:, half, :], PREDICT_LINE, ALU.is_gt)
             nc.vector.tensor_tensor(conf_p[:, half, :], conf[:, half, :], p_bf[:, half, :], ALU.mult)
+            if half == early:
+                subtract(0)
+                find_hit(0)
+                find_dec(0)
             nc.vector.tensor_tensor(conf_rest[:, half, :], conf[:, half, :], conf_p[:, half, :], ALU.subtract)
 
-        conf_t = banks.tile([P, NB, P], BF16, name="conf_t", tag="bank")
-        for n in range(NB):
-            nc.tensor.transpose(conf_t[:, n, :], conf[:, n, :], identity_bf[:])
         count = banks.tile([P, 1], F32, name="count", tag="bank")
         for k in range(NB):
             nc.tensor.matmul(count[:], conf[:, k, :], all_ones[:, 0:1], start=k == 0, stop=k == NB - 1)
+        conf_t = banks.tile([P, NB, P], BF16, name="conf_t", tag="bank")
+        for n in range(NB):
+            nc.tensor.transpose(conf_t[:, n, :], conf[:, n, :], identity_bf[:])
 
         inv_rel_t = held.tile([P, NB, P], F32, name="inv_rel_t")
         inv_rel = held.tile([P, NB, N], F32, name="inv_rel")
         den = held.tile([P, 2], F32, name="den")
         inv = held.tile([P, 2], F32, name="inv")
         slope = held.tile([P, 1], F32, name="slope")
-        backs = []
 
         nc.vector.tensor_single_scalar(den[:, 0:1], count[:], 1.0, ALU.add)
         nc.vector.tensor_single_scalar(den[:, 1:2], count[:], 1.0, ALU.max)
         nc.vector.reciprocal(inv[:], den[:])
-        nc.vector.tensor_tensor(slope[:], inv[:, 0:1], inv[:, 1:2], ALU.mult)
+        nc.gpsimd.tensor_tensor(slope[:], inv[:, 0:1], inv[:, 1:2], ALU.mult)
 
         def spread_inverse():
             nc.scalar.activation(inv_rel_t[:], conf_t[:], IDENTITY, bias=inv[:, 0:1], scale=slope[:, 0:1])
 
         def flip_back():
             for h in range(NB // BANK):
-                back = banks.tile([P, BANK, N], F32, name="back", tag="bank")
+                back = backs.tile([P, BANK, N], F32, name="back")
                 for i in range(BANK):
                     nc.tensor.transpose(back[:, i, :], inv_rel_t[:, h * BANK + i, :], identity[:])
-                backs.append(back)
-
-        def copy_back():
-            for h in range(NB // BANK):
-                nc.scalar.copy(inv_rel[:, h * BANK : (h + 1) * BANK, :], backs[h][:])
+                nc.scalar.copy(inv_rel[:, h * BANK : (h + 1) * BANK, :], back[:])
 
         n_pieces = len(pieces)
         for t in range(1, AHEAD):
@@ -203,11 +208,9 @@ def tile_labelsmoothloss_kernel(tc, base, p, adj, prob, offs, out):
                 weigh(step - 2)
             if step == n_pieces // 2:
                 flip_back()
-            weighed = step - 4
+            weighed = step - 2
             if 0 <= weighed < n_pieces - 1 and pieces[weighed][1] + pieces[weighed][2] == NB:
                 collect(pieces[weighed][0])
-            if step == n_pieces - AHEAD + 1:
-                copy_back()
         for n in range(NB):
             if n == NB - GROUP:
                 collect(NB // GROUP - 1)

@@ -14,8 +14,8 @@ BANK = HALF // P
 HALF_BLOCKS = NB // 2
 W = 512
 GROUP = W // P
-DEPTH = C // W
-PIECES = NB // DEPTH
+DEPTH = 2
+LATE = 3
 PREDICT_LINE = 0.6
 RELATION_GAP = 0.05
 TOP = 2.0
@@ -35,7 +35,7 @@ def tile_labelsmoothloss_kernel(tc, base, p, adj, prob, offs, out):
 
     with (
         tc.tile_pool(name="held", bufs=1) as held,
-        tc.tile_pool(name="loads", bufs=NB + 2) as loads,
+        tc.tile_pool(name="loads", bufs=NB + 4) as loads,
         tc.tile_pool(name="work", bufs=8) as work,
         tc.psum_pool(name="banks", bufs=7) as banks,
         tc.psum_pool(name="backs", bufs=1) as backs,
@@ -48,12 +48,11 @@ def tile_labelsmoothloss_kernel(tc, base, p, adj, prob, offs, out):
         nc.vector.memset(all_ones[:], 1.0)
         p_sb = held.tile([P, NB, N], F32, name="p_sb")
         early, late = slice(0, HALF_BLOCKS), slice(HALF_BLOCKS, NB)
-        nc.sync.dma_start(p_sb[:, early, :], p_blocks[:, early, :])
-        pieces = [(g, i * DEPTH, DEPTH) for g in range(C // W) for i in range(PIECES)]
         pieces = (
-            [(0, 0, DEPTH // 2), (0, DEPTH // 2, DEPTH // 2)]
-            + pieces[1:-1]
-            + [(C // W - 1, NB - DEPTH, DEPTH // 2), (C // W - 1, NB - DEPTH // 2, DEPTH // 2)]
+            [(0, k, 1) for k in range(NB - DEPTH)]
+            + [(0, NB - DEPTH, DEPTH)]
+            + [(1, k, DEPTH) for k in range(0, NB - DEPTH, DEPTH)]
+            + [(1, k, 1) for k in range(NB - DEPTH, NB)]
         )
         adj_pieces, windows = [], []
         for g, first, blocks in pieces:
@@ -61,6 +60,8 @@ def tile_labelsmoothloss_kernel(tc, base, p, adj, prob, offs, out):
             nc.sync.dma_start(adj_c[:], adj_blocks[:, first : first + blocks, g * W : (g + 1) * W])
             adj_pieces.append(adj_c)
             if len(adj_pieces) == 1:
+                nc.sync.dma_start(p_sb[:, early, :], p_blocks[:, early, :])
+            if len(adj_pieces) == LATE:
                 nc.sync.dma_start(p_sb[:, late, :], p_blocks[:, late, :])
         offsets = held.tile([P, N // 16], U16, name="offsets")
         nc.sync.dma_start(offsets[:], offs)
@@ -151,24 +152,11 @@ def tile_labelsmoothloss_kernel(tc, base, p, adj, prob, offs, out):
         conf = held.tile([P, NB, N], BF16, name="conf")
         conf_p = held.tile([P, NB, N], BF16, name="conf_p")
         conf_rest = held.tile([P, NB, N], BF16, name="conf_rest")
-        for half in (early, late):
+        def take_p(half):
             nc.vector.tensor_single_scalar(conf[:, half, :], p_sb[:, half, :], PREDICT_LINE, ALU.is_gt)
-            if half == early:
-                round_off(0)
             nc.scalar.activation(p_bf[:, half, :], p_sb[:, half, :], COPY)
             nc.vector.tensor_tensor(conf_p[:, half, :], conf[:, half, :], p_bf[:, half, :], ALU.mult)
-            if half == early:
-                subtract(0)
-                find_hit(0)
-                find_dec(0)
             nc.vector.tensor_tensor(conf_rest[:, half, :], conf[:, half, :], conf_p[:, half, :], ALU.subtract)
-
-        count = banks.tile([P, 1], F32, name="count", tag="bank")
-        for k in range(NB):
-            nc.tensor.matmul(count[:], conf[:, k, :], all_ones[:, 0:1], start=k == 0, stop=k == NB - 1)
-        conf_t = banks.tile([P, NB, P], BF16, name="conf_t", tag="bank")
-        for n in range(NB):
-            nc.tensor.transpose(conf_t[:, n, :], conf[:, n, :], identity_bf[:])
 
         inv_rel_t = held.tile([P, NB, P], F32, name="inv_rel_t")
         inv_rel = held.tile([P, NB, N], F32, name="inv_rel")
@@ -176,12 +164,20 @@ def tile_labelsmoothloss_kernel(tc, base, p, adj, prob, offs, out):
         inv = held.tile([P, 2], F32, name="inv")
         slope = held.tile([P, 1], F32, name="slope")
 
-        nc.vector.tensor_single_scalar(den[:, 0:1], count[:], 1.0, ALU.add)
-        nc.vector.tensor_single_scalar(den[:, 1:2], count[:], 1.0, ALU.max)
-        nc.vector.reciprocal(inv[:], den[:])
-        nc.gpsimd.tensor_tensor(slope[:], inv[:, 0:1], inv[:, 1:2], ALU.mult)
+        def find_inverse():
+            count = banks.tile([P, 1], F32, name="count", tag="bank")
+            for k in range(NB):
+                nc.tensor.matmul(count[:], conf[:, k, :], all_ones[:, 0:1], start=k == 0, stop=k == NB - 1)
+            conf_t = banks.tile([P, NB, P], BF16, name="conf_t", tag="bank")
+            for n in range(NB):
+                nc.tensor.transpose(conf_t[:, n, :], conf[:, n, :], identity_bf[:])
+            nc.vector.tensor_single_scalar(den[:, 0:1], count[:], 1.0, ALU.add)
+            nc.vector.tensor_single_scalar(den[:, 1:2], count[:], 1.0, ALU.max)
+            nc.vector.reciprocal(inv[:], den[:])
+            nc.gpsimd.tensor_tensor(slope[:], inv[:, 0:1], inv[:, 1:2], ALU.mult)
+            return conf_t
 
-        def spread_inverse():
+        def spread_inverse(conf_t):
             nc.scalar.activation(inv_rel_t[:], conf_t[:], IDENTITY, bias=inv[:, 0:1], scale=slope[:, 0:1])
 
         def flip_back():
@@ -192,21 +188,26 @@ def tile_labelsmoothloss_kernel(tc, base, p, adj, prob, offs, out):
                 nc.scalar.copy(inv_rel[:, h * BANK : (h + 1) * BANK, :], back[:])
 
         n_pieces = len(pieces)
-        for t in range(1, AHEAD):
-            round_off(t)
+        round_off(0)
+        take_p(early)
+        round_off(1)
         for step in range(n_pieces + 2):
             if step + AHEAD < n_pieces:
                 round_off(step + AHEAD)
-            if step == 1:
-                spread_inverse()
-            if 1 <= step < n_pieces:
+            if step < n_pieces:
                 subtract(step)
-            if 1 <= step - 1 < n_pieces:
+            if step == LATE:
+                take_p(late)
+            if step == LATE + 1:
+                conf_t = find_inverse()
+            if step == n_pieces // 2 + 1:
+                spread_inverse(conf_t)
+            if 0 <= step - 1 < n_pieces:
                 find_hit(step - 1)
                 find_dec(step - 1)
             if 0 <= step - 2 < n_pieces:
                 weigh(step - 2)
-            if step == n_pieces // 2:
+            if step == n_pieces - AHEAD:
                 flip_back()
             weighed = step - 2
             if 0 <= weighed < n_pieces - 1 and pieces[weighed][1] + pieces[weighed][2] == NB:

@@ -49,15 +49,15 @@ def tile_labelsmoothloss_kernel(tc, base, p, adj, prob, offs, out):
         p_sb = held.tile([P, NB, N], F32, name="p_sb")
         early, late = slice(0, HALF_BLOCKS), slice(HALF_BLOCKS, NB)
         pieces = (
-            [(0, k, 1) for k in range(NB - DEPTH)]
-            + [(0, NB - DEPTH, DEPTH)]
-            + [(1, k, DEPTH) for k in range(0, NB - DEPTH, DEPTH)]
-            + [(1, k, 1) for k in range(NB - DEPTH, NB)]
+            [(0, W, k, 1) for k in range(NB - DEPTH)]
+            + [(0, W, NB - DEPTH, DEPTH)]
+            + [(W, W, k, DEPTH) for k in range(0, NB - DEPTH, DEPTH)]
+            + [(c, W // 2, NB - DEPTH, DEPTH) for c in (W, W + W // 2)]
         )
         adj_pieces, windows = [], []
-        for g, first, blocks in pieces:
-            adj_c = loads.tile([P, blocks, W], F32, name="adj_c")
-            nc.sync.dma_start(adj_c[:], adj_blocks[:, first : first + blocks, g * W : (g + 1) * W])
+        for begin, width, first, blocks in pieces:
+            adj_c = loads.tile([P, blocks, width], F32, name="adj_c")
+            nc.sync.dma_start(adj_c[:], adj_blocks[:, first : first + blocks, begin : begin + width])
             adj_pieces.append(adj_c)
             if len(adj_pieces) == 1:
                 nc.sync.dma_start(p_sb[:, early, :], p_blocks[:, early, :])
@@ -88,57 +88,65 @@ def tile_labelsmoothloss_kernel(tc, base, p, adj, prob, offs, out):
             priors_bf[g] = banks.tile([P, W], BF16, name="repeated", tag="bank")
             nc.tensor.matmul(priors_bf[g][:], all_ones[:], prior_rows_bf[:, columns], start=True, stop=True)
 
+        def shape(t):
+            begin, width, first, blocks = pieces[t]
+            return [P, blocks, width]
+
         def round_off(t):
-            g, first, blocks = pieces[t]
-            adj_bfs[t] = loads.tile([P, blocks, W], BF16, name="adj_bf")
+            adj_bfs[t] = loads.tile(shape(t), BF16, name="adj_bf")
             if t == 0:
                 nc.vector.tensor_single_scalar(adj_bfs[t][:], adj_pieces[t][:], SCALE, ALU.mult)
             else:
                 nc.scalar.activation(adj_bfs[t][:], adj_pieces[t][:], COPY, scale=SCALE)
 
         def subtract(t):
-            g, first, blocks = pieces[t]
-            diffs[t] = work.tile([P, blocks, W], BF16, name="diff")
+            begin, width, first, blocks = pieces[t]
+            prior = priors_bf[begin // W][:, begin % W : begin % W + width]
+            diffs[t] = work.tile([P, blocks, width], BF16, name="diff")
             nc.vector.tensor_tensor(
-                diffs[t][:], adj_bfs[t][:], priors_bf[g][:].unsqueeze(1).to_broadcast([P, blocks, W]), ALU.subtract
+                diffs[t][:], adj_bfs[t][:], prior.unsqueeze(1).to_broadcast([P, blocks, width]), ALU.subtract
             )
 
         def find_dec(t):
-            decs[t] = work.tile([P, pieces[t][2], W], BF16, name="dec")
+            decs[t] = work.tile(shape(t), BF16, name="dec")
             nc.vector.tensor_scalar(decs[t][:], diffs[t][:], -TOP, SUM_SCALE, ALU.is_lt, ALU.mult)
 
         def find_hit(t):
-            hits[t] = work.tile([P, pieces[t][2], W], BF16, name="hit")
+            hits[t] = work.tile(shape(t), BF16, name="hit")
             nc.vector.tensor_single_scalar(
                 hits[t][:].bitcast(I32), diffs[t][:].bitcast(I32), TOP_EXPONENT_BITS, ALU.bitwise_and
             )
 
+        def open_sums(g):
+            for n in range(g * GROUP, (g + 1) * GROUP):
+                nums_ps[n] = banks.tile([P, N], F32, name="num_ps", tag="bank")
+
+        def add_p(g):
+            for n in range(g * GROUP, (g + 1) * GROUP):
+                nc.tensor.matmul(nums_ps[n][:], scaled_identity[:], p_sb[:, n, :], start=g > 0, stop=False)
+
         def weigh(t):
-            g, first, blocks = pieces[t]
-            hit_adj = work.tile([P, blocks, W], BF16, name="hit_adj")
+            begin, width, first, blocks = pieces[t]
+            hit_adj = work.tile(shape(t), BF16, name="hit_adj")
             nc.vector.tensor_tensor(hit_adj[:], hits[t][:], adj_bfs[t][:], ALU.mult)
-            p_joins = DEPTH if g == 0 else 0
-            for m in range(GROUP):
-                n = g * GROUP + m
-                if first == 0:
-                    nums_ps[n] = banks.tile([P, N], F32, name="num_ps", tag="bank")
-                if first == p_joins:
-                    nc.tensor.matmul(nums_ps[n][:], scaled_identity[:], p_sb[:, n, :], start=first == 0, stop=False)
+            for m in range(width // P):
+                n = begin // P + m
                 for b in range(blocks):
                     k = first + b
                     nc.tensor.matmul(
                         nums_ps[n][:],
                         hit_adj[:, b, m * P : (m + 1) * P],
                         conf_p[:, k, :],
-                        start=k == 0 and p_joins > 0,
+                        start=begin < W and k == 0,
                         stop=False,
                     )
                     nc.tensor.matmul(
                         nums_ps[n][:], decs[t][:, b, m * P : (m + 1) * P], conf_rest[:, k, :], start=False, stop=k == NB - 1
                     )
 
-        def collect(g):
-            for n in range(g * GROUP, (g + 1) * GROUP):
+        def collect(t):
+            begin, width, first, blocks = pieces[t]
+            for n in range(begin // P, (begin + width) // P):
                 nums[n] = loads.tile([P, N], F32, name="num")
                 nc.scalar.activation(nums[n][:], nums_ps[n][:], COPY, scale=1.0 / SUM_SCALE)
 
@@ -196,23 +204,28 @@ def tile_labelsmoothloss_kernel(tc, base, p, adj, prob, offs, out):
                 round_off(step + AHEAD)
             if step < n_pieces:
                 subtract(step)
+            if step == 1:
+                open_sums(0)
             if step == LATE:
                 take_p(late)
             if step == LATE + 1:
                 conf_t = find_inverse()
-            if step == n_pieces // 2 + 1:
+            if step == LATE + 3:
                 spread_inverse(conf_t)
+                add_p(0)
+                flip_back()
+                open_sums(1)
+                add_p(1)
             if 0 <= step - 1 < n_pieces:
                 find_hit(step - 1)
                 find_dec(step - 1)
             if 0 <= step - 2 < n_pieces:
                 weigh(step - 2)
-            if step == n_pieces - AHEAD:
-                flip_back()
             weighed = step - 2
-            if 0 <= weighed < n_pieces - 1 and pieces[weighed][1] + pieces[weighed][2] == NB:
-                collect(pieces[weighed][0])
+            if 0 <= weighed < n_pieces - 1 and pieces[weighed][2] + pieces[weighed][3] == NB:
+                collect(weighed)
+        last_begin = pieces[-1][0]
         for n in range(NB):
-            if n == NB - GROUP:
-                collect(NB // GROUP - 1)
+            if n == last_begin // P:
+                collect(n_pieces - 1)
             place(n)

@@ -15,13 +15,14 @@ HALF_BLOCKS = NB // 2
 W = 512
 GROUP = W // P
 DEPTH = 2
-LATE = 3
+LATE = 2
 PREDICT_LINE = 0.6
 RELATION_GAP = 0.05
 TOP = 2.0
 SCALE = TOP / RELATION_GAP
 TOP_EXPONENT_BITS = 0x40004000
 SUM_SCALE = TOP * SCALE
+TINY = 2.0**-30
 AHEAD = 2
 
 FLOPS = 2 * 2 * C * C * N
@@ -49,19 +50,26 @@ def tile_labelsmoothloss_kernel(tc, base, p, adj, prob, offs, out):
         p_sb = held.tile([P, NB, N], F32, name="p_sb")
         early, late = slice(0, HALF_BLOCKS), slice(HALF_BLOCKS, NB)
         pieces = (
-            [(0, W, k, 1) for k in range(NB - DEPTH)]
-            + [(0, W, NB - DEPTH, DEPTH)]
+            [(0, W, k, 1) for k in range(DEPTH)]
+            + [(0, W, k, DEPTH) for k in range(DEPTH, NB, DEPTH)]
             + [(W, W, k, DEPTH) for k in range(0, NB - DEPTH, DEPTH)]
             + [(c, W // 2, NB - DEPTH, DEPTH) for c in (W, W + W // 2)]
         )
+
+        def parts(t):
+            begin, width, first, blocks = pieces[t]
+            return [slice(b, b + 1) for b in range(blocks)] if begin < W else [slice(0, blocks)]
+
         adj_pieces, windows = [], []
-        for begin, width, first, blocks in pieces:
+        for t, (begin, width, first, blocks) in enumerate(pieces):
             adj_c = loads.tile([P, blocks, width], F32, name="adj_c")
-            nc.sync.dma_start(adj_c[:], adj_blocks[:, first : first + blocks, begin : begin + width])
+            for part in parts(t):
+                rows = slice(first + part.start, first + part.stop)
+                nc.sync.dma_start(adj_c[:, part, :], adj_blocks[:, rows, begin : begin + width])
             adj_pieces.append(adj_c)
-            if len(adj_pieces) == 1:
+            if t == 0:
                 nc.sync.dma_start(p_sb[:, early, :], p_blocks[:, early, :])
-            if len(adj_pieces) == LATE:
+            if t == LATE:
                 nc.sync.dma_start(p_sb[:, late, :], p_blocks[:, late, :])
         offsets = held.tile([P, N // 16], U16, name="offsets")
         nc.sync.dma_start(offsets[:], offs)
@@ -97,15 +105,20 @@ def tile_labelsmoothloss_kernel(tc, base, p, adj, prob, offs, out):
             if t == 0:
                 nc.vector.tensor_single_scalar(adj_bfs[t][:], adj_pieces[t][:], SCALE, ALU.mult)
             else:
-                nc.scalar.activation(adj_bfs[t][:], adj_pieces[t][:], COPY, scale=SCALE)
+                for part in parts(t):
+                    nc.scalar.activation(adj_bfs[t][:, part, :], adj_pieces[t][:, part, :], COPY, scale=SCALE)
 
         def subtract(t):
             begin, width, first, blocks = pieces[t]
             prior = priors_bf[begin // W][:, begin % W : begin % W + width]
             diffs[t] = work.tile([P, blocks, width], BF16, name="diff")
-            nc.vector.tensor_tensor(
-                diffs[t][:], adj_bfs[t][:], prior.unsqueeze(1).to_broadcast([P, blocks, width]), ALU.subtract
-            )
+            for part in parts(t):
+                nc.vector.tensor_tensor(
+                    diffs[t][:, part, :],
+                    adj_bfs[t][:, part, :],
+                    prior.unsqueeze(1).to_broadcast([P, part.stop - part.start, width]),
+                    ALU.subtract,
+                )
 
         def find_dec(t):
             decs[t] = work.tile(shape(t), BF16, name="dec")
@@ -161,8 +174,9 @@ def tile_labelsmoothloss_kernel(tc, base, p, adj, prob, offs, out):
         conf_p = held.tile([P, NB, N], BF16, name="conf_p")
         conf_rest = held.tile([P, NB, N], BF16, name="conf_rest")
         def take_p(half):
-            nc.vector.tensor_single_scalar(conf[:, half, :], p_sb[:, half, :], PREDICT_LINE, ALU.is_gt)
             nc.scalar.activation(p_bf[:, half, :], p_sb[:, half, :], COPY)
+            compared = p_sb if half == early else p_bf
+            nc.vector.tensor_single_scalar(conf[:, half, :], compared[:, half, :], PREDICT_LINE, ALU.is_gt)
             nc.vector.tensor_tensor(conf_p[:, half, :], conf[:, half, :], p_bf[:, half, :], ALU.mult)
             nc.vector.tensor_tensor(conf_rest[:, half, :], conf[:, half, :], conf_p[:, half, :], ALU.subtract)
 
@@ -179,8 +193,8 @@ def tile_labelsmoothloss_kernel(tc, base, p, adj, prob, offs, out):
             conf_t = banks.tile([P, NB, P], BF16, name="conf_t", tag="bank")
             for n in range(NB):
                 nc.tensor.transpose(conf_t[:, n, :], conf[:, n, :], identity_bf[:])
-            nc.vector.tensor_single_scalar(den[:, 0:1], count[:], 1.0, ALU.add)
-            nc.vector.tensor_single_scalar(den[:, 1:2], count[:], 1.0, ALU.max)
+            nc.scalar.activation(den[:, 0:1], count[:], COPY, bias=1.0)
+            nc.scalar.activation(den[:, 1:2], count[:], COPY, bias=TINY)
             nc.vector.reciprocal(inv[:], den[:])
             nc.gpsimd.tensor_tensor(slope[:], inv[:, 0:1], inv[:, 1:2], ALU.mult)
             return conf_t
@@ -208,9 +222,8 @@ def tile_labelsmoothloss_kernel(tc, base, p, adj, prob, offs, out):
                 open_sums(0)
             if step == LATE:
                 take_p(late)
-            if step == LATE + 1:
                 conf_t = find_inverse()
-            if step == LATE + 3:
+            if step == LATE + 2:
                 spread_inverse(conf_t)
                 add_p(0)
                 flip_back()

import concourse.mybir as mybir
from concourse.masks import make_identity

F32, BF16, U16, I32 = mybir.dt.float32, mybir.dt.bfloat16, mybir.dt.uint16, mybir.dt.int32
ALU = mybir.AluOpType
ACT = mybir.ActivationFunctionType
COPY, IDENTITY = ACT.Copy, ACT.Identity

P = 128
C, S, N = 1024, 256, 128
NB = C // P
HALF = 512
BANK = HALF // P
HALF_BLOCKS = NB // 2
W = 512
GROUP = W // P
DEPTH = 2
LATE = 2
PREDICT_LINE = 0.6
RELATION_GAP = 0.05
TOP = 2.0
SCALE = TOP / RELATION_GAP
TOP_EXPONENT_BITS = 0x40004000
SUM_SCALE = TOP * SCALE
TINY = 2.0**-30
AHEAD = 2

FLOPS = 2 * 2 * C * C * N


def tile_labelsmoothloss_kernel(tc, base, p, adj, prob, offs, out):
    nc = tc.nc
    p_blocks = p.rearrange("(b q) j -> q b j", q=P)
    adj_blocks = adj.rearrange("(b q) c -> q b c", q=P)
    prior_row = prob.rearrange("c o -> o c")

    with (
        tc.tile_pool(name="held", bufs=1) as held,
        tc.tile_pool(name="loads", bufs=NB + 4) as loads,
        tc.tile_pool(name="work", bufs=8) as work,
        tc.psum_pool(name="banks", bufs=7) as banks,
        tc.psum_pool(name="backs", bufs=1) as backs,
    ):
        priors = held.tile([1, C], F32, name="priors")
        nc.sync.dma_start(priors[:], prior_row)
        prior_rows_bf = held.tile([P, C], BF16, name="prior_rows_bf")
        nc.vector.memset(prior_rows_bf[:], 0.0)
        all_ones = held.tile([P, P], BF16, name="all_ones")
        nc.vector.memset(all_ones[:], 1.0)
        p_sb = held.tile([P, NB, N], F32, name="p_sb")
        early, late = slice(0, HALF_BLOCKS), slice(HALF_BLOCKS, NB)
        pieces = (
            [(0, W, k, 1) for k in range(DEPTH)]
            + [(0, W, k, DEPTH) for k in range(DEPTH, NB, DEPTH)]
            + [(W, W, k, DEPTH) for k in range(0, NB - DEPTH, DEPTH)]
            + [(c, W // 2, NB - DEPTH, DEPTH) for c in (W, W + W // 2)]
        )

        def parts(t):
            begin, width, first, blocks = pieces[t]
            return [slice(b, b + 1) for b in range(blocks)] if begin < W else [slice(0, blocks)]

        adj_pieces, windows = [], []
        for t, (begin, width, first, blocks) in enumerate(pieces):
            adj_c = loads.tile([P, blocks, width], F32, name="adj_c")
            for part in parts(t):
                rows = slice(first + part.start, first + part.stop)
                nc.sync.dma_start(adj_c[:, part, :], adj_blocks[:, rows, begin : begin + width])
            adj_pieces.append(adj_c)
            if t == 0:
                nc.sync.dma_start(p_sb[:, early, :], p_blocks[:, early, :])
            if t == LATE:
                nc.sync.dma_start(p_sb[:, late, :], p_blocks[:, late, :])
        offsets = held.tile([P, N // 16], U16, name="offsets")
        nc.sync.dma_start(offsets[:], offs)
        for n in range(NB):
            window = loads.tile([P, S], F32, name="window")
            nc.sync.dma_start(window[:], base[n * P : (n + 1) * P, :])
            windows.append(window)

        identity_bf = held.tile([P, P], BF16, name="identity_bf")
        make_identity(nc, identity_bf[:])
        identity = held.tile([P, P], F32, name="identity")
        nc.gpsimd.tensor_copy(identity[:], identity_bf[:])
        scaled_identity = held.tile([P, P], F32, name="scaled_identity")
        nc.gpsimd.tensor_single_scalar(scaled_identity[:], identity_bf[:], SUM_SCALE, ALU.mult)
        scratch = held.tile([P, 1], F32, name="scratch")
        nc.vector.memset(scratch[:], 0.0)
        nc.scalar.activation(scratch[:], scratch[:], COPY)

        priors_bf, adj_bfs, diffs, decs, hits, nums_ps, nums = {}, {}, {}, {}, {}, {}, {}

        def repeat_priors(g):
            columns = slice(g * W, (g + 1) * W)
            nc.vector.tensor_single_scalar(prior_rows_bf[0:1, columns], priors[:, columns], SCALE, ALU.mult)
            priors_bf[g] = banks.tile([P, W], BF16, name="repeated", tag="bank")
            nc.tensor.matmul(priors_bf[g][:], all_ones[:], prior_rows_bf[:, columns], start=True, stop=True)

        def shape(t):
            begin, width, first, blocks = pieces[t]
            return [P, blocks, width]

        def round_off(t):
            adj_bfs[t] = loads.tile(shape(t), BF16, name="adj_bf")
            if t == 0:
                nc.vector.tensor_single_scalar(adj_bfs[t][:], adj_pieces[t][:], SCALE, ALU.mult)
            else:
                for part in parts(t):
                    nc.scalar.activation(adj_bfs[t][:, part, :], adj_pieces[t][:, part, :], COPY, scale=SCALE)

        def subtract(t):
            begin, width, first, blocks = pieces[t]
            prior = priors_bf[begin // W][:, begin % W : begin % W + width]
            diffs[t] = work.tile([P, blocks, width], BF16, name="diff")
            for part in parts(t):
                nc.vector.tensor_tensor(
                    diffs[t][:, part, :],
                    adj_bfs[t][:, part, :],
                    prior.unsqueeze(1).to_broadcast([P, part.stop - part.start, width]),
                    ALU.subtract,
                )

        def find_dec(t):
            decs[t] = work.tile(shape(t), BF16, name="dec")
            nc.vector.tensor_scalar(decs[t][:], diffs[t][:], -TOP, SUM_SCALE, ALU.is_lt, ALU.mult)

        def find_hit(t):
            hits[t] = work.tile(shape(t), BF16, name="hit")
            nc.vector.tensor_single_scalar(
                hits[t][:].bitcast(I32), diffs[t][:].bitcast(I32), TOP_EXPONENT_BITS, ALU.bitwise_and
            )

        def open_sums(g):
            for n in range(g * GROUP, (g + 1) * GROUP):
                nums_ps[n] = banks.tile([P, N], F32, name="num_ps", tag="bank")

        def add_p(g):
            for n in range(g * GROUP, (g + 1) * GROUP):
                nc.tensor.matmul(nums_ps[n][:], scaled_identity[:], p_sb[:, n, :], start=g > 0, stop=False)

        def weigh(t):
            begin, width, first, blocks = pieces[t]
            hit_adj = work.tile(shape(t), BF16, name="hit_adj")
            nc.vector.tensor_tensor(hit_adj[:], hits[t][:], adj_bfs[t][:], ALU.mult)
            for m in range(width // P):
                n = begin // P + m
                for b in range(blocks):
                    k = first + b
                    nc.tensor.matmul(
                        nums_ps[n][:],
                        hit_adj[:, b, m * P : (m + 1) * P],
                        conf_p[:, k, :],
                        start=begin < W and k == 0,
                        stop=False,
                    )
                    nc.tensor.matmul(
                        nums_ps[n][:], decs[t][:, b, m * P : (m + 1) * P], conf_rest[:, k, :], start=False, stop=k == NB - 1
                    )

        def collect(t):
            begin, width, first, blocks = pieces[t]
            for n in range(begin // P, (begin + width) // P):
                nums[n] = loads.tile([P, N], F32, name="num")
                nc.scalar.activation(nums[n][:], nums_ps[n][:], COPY, scale=1.0 / SUM_SCALE)

        def place(n):
            nc.vector.tensor_tensor(windows[n][:].indirect(offsets[:]), nums[n][:], inv_rel[:, n, :], ALU.mult)
            nc.sync.dma_start(out[n * P : (n + 1) * P, :], windows[n][:])

        repeat_priors(0)
        repeat_priors(1)
        p_bf = held.tile([P, NB, N], BF16, name="p_bf")
        conf = held.tile([P, NB, N], BF16, name="conf")
        conf_p = held.tile([P, NB, N], BF16, name="conf_p")
        conf_rest = held.tile([P, NB, N], BF16, name="conf_rest")
        def take_p(half):
            nc.scalar.activation(p_bf[:, half, :], p_sb[:, half, :], COPY)
            compared = p_sb if half == early else p_bf
            nc.vector.tensor_single_scalar(conf[:, half, :], compared[:, half, :], PREDICT_LINE, ALU.is_gt)
            nc.vector.tensor_tensor(conf_p[:, half, :], conf[:, half, :], p_bf[:, half, :], ALU.mult)
            nc.vector.tensor_tensor(conf_rest[:, half, :], conf[:, half, :], conf_p[:, half, :], ALU.subtract)

        inv_rel_t = held.tile([P, NB, P], F32, name="inv_rel_t")
        inv_rel = held.tile([P, NB, N], F32, name="inv_rel")
        den = held.tile([P, 2], F32, name="den")
        inv = held.tile([P, 2], F32, name="inv")
        slope = held.tile([P, 1], F32, name="slope")

        def find_inverse():
            count = banks.tile([P, 1], F32, name="count", tag="bank")
            for k in range(NB):
                nc.tensor.matmul(count[:], conf[:, k, :], all_ones[:, 0:1], start=k == 0, stop=k == NB - 1)
            conf_t = banks.tile([P, NB, P], BF16, name="conf_t", tag="bank")
            for n in range(NB):
                nc.tensor.transpose(conf_t[:, n, :], conf[:, n, :], identity_bf[:])
            nc.scalar.activation(den[:, 0:1], count[:], COPY, bias=1.0)
            nc.scalar.activation(den[:, 1:2], count[:], COPY, bias=TINY)
            nc.vector.reciprocal(inv[:], den[:])
            nc.gpsimd.tensor_tensor(slope[:], inv[:, 0:1], inv[:, 1:2], ALU.mult)
            return conf_t

        def spread_inverse(conf_t):
            nc.scalar.activation(inv_rel_t[:], conf_t[:], IDENTITY, bias=inv[:, 0:1], scale=slope[:, 0:1])

        def flip_back():
            for h in range(NB // BANK):
                back = backs.tile([P, BANK, N], F32, name="back")
                for i in range(BANK):
                    nc.tensor.transpose(back[:, i, :], inv_rel_t[:, h * BANK + i, :], identity[:])
                nc.scalar.copy(inv_rel[:, h * BANK : (h + 1) * BANK, :], back[:])

        n_pieces = len(pieces)
        round_off(0)
        take_p(early)
        round_off(1)
        for step in range(n_pieces + 2):
            if step + AHEAD < n_pieces:
                round_off(step + AHEAD)
            if step < n_pieces:
                subtract(step)
            if step == 1:
                open_sums(0)
            if step == LATE:
                take_p(late)
                conf_t = find_inverse()
            if step == LATE + 2:
                spread_inverse(conf_t)
                add_p(0)
                flip_back()
                open_sums(1)
                add_p(1)
            if 0 <= step - 1 < n_pieces:
                find_hit(step - 1)
                find_dec(step - 1)
            if 0 <= step - 2 < n_pieces:
                weigh(step - 2)
            weighed = step - 2
            if 0 <= weighed < n_pieces - 1 and pieces[weighed][2] + pieces[weighed][3] == NB:
                collect(weighed)
        last_begin = pieces[-1][0]
        for n in range(NB):
            if n == last_begin // P:
                collect(n_pieces - 1)
            place(n)
